import numpy as np
import ml_dtypes


def mxq(x, axis, fmt="e4m3"):
    dtype, down = {"e4m3": (ml_dtypes.float8_e4m3fn, 7), "e5m2": (ml_dtypes.float8_e5m2, 14)}[fmt]
    v = np.moveaxis(np.asarray(x, np.float32).astype(ml_dtypes.bfloat16).astype(np.float64), axis, -1)
    blocks = v.reshape(v.shape[:-1] + (-1, 32))
    amax = np.abs(blocks).max(-1, keepdims=True)
    byte = np.maximum(np.where(amax > 0, np.frexp(amax)[1] - 1 + 127, 0) - down, 1)
    scale = np.exp2(byte - 127.0)
    codes = (blocks / scale).astype(np.float32).astype(dtype).astype(np.float64)
    return np.moveaxis((codes * scale).reshape(v.shape), -1, axis)


WIDE = False


def mx_kscale(k):
    if not WIDE:
        return np.ones(k)
    levels = np.array([30, -30])
    if k % 512:
        return np.exp2(np.random.permutation(np.resize(levels, k // 32))).repeat(32)
    a = np.empty((k // 512, 16))
    for p in range(k // 512):
        a[p, :8] = np.random.permutation(np.resize(levels, 8))
        for g in range(8):
            far = levels[np.abs(levels - a[p, g]) >= 10]
            a[p, g + 8] = far[np.random.randint(len(far))]
    return np.exp2(a.ravel()).repeat(32)


BF16 = ml_dtypes.bfloat16


def bf(x):
    return np.asarray(x, np.float32).astype(BF16)


def f64(x):
    return np.asarray(x).astype(np.float64)


B, N, D, H, DH = 4, 640, 1024, 16, 64
R = 2 * DH
EPS = 1e-12
BASE = 10000.0


def l2norm(t):
    n = np.sqrt(np.sum(t * t, axis=-1, keepdims=True))
    return t / np.maximum(n, EPS)


def rotate_half(t):
    t1, t2 = np.split(t, 2, axis=-1)
    return np.concatenate([-t2, t1], axis=-1)


def rope_tables():
    inv_freq = 1.0 / (BASE ** (np.arange(0, R, 2) / R))
    freqs = np.outer(np.arange(N), inv_freq)
    emb = np.concatenate([freqs, freqs], axis=-1)
    return np.cos(emb), np.sin(emb)


def setup_inputs():
    s, t = mx_kscale(D), mx_kscale(D)
    g = 0.5 * np.sqrt(DH)
    return {
        "x": bf(np.random.standard_normal((B, N, D)) * s),
        "a": bf(np.random.standard_normal((B, N, D)) * t),
        "Wq_x": bf(np.random.standard_normal((H * DH, D)) / np.sqrt(D) / s),
        "Wq_a": bf(np.random.standard_normal((H * DH, D)) / np.sqrt(D) / t),
        "qx_scale": bf(g * (1.0 + 0.1 * np.random.standard_normal((H, 1, DH)))),
        "qa_scale": bf(g * (1.0 + 0.1 * np.random.standard_normal((H, 1, DH)))),
    }


def reference(x, a, Wq_x, Wq_a, qx_scale, qa_scale):
    q_x = mxq(f64(x), 2, "e5m2") @ mxq(f64(Wq_x), 1, "e5m2").T
    q_a = mxq(f64(a), 2, "e5m2") @ mxq(f64(Wq_a), 1, "e5m2").T
    q_x = q_x.reshape(B, N, H, DH).transpose(0, 2, 1, 3)
    q_a = q_a.reshape(B, N, H, DH).transpose(0, 2, 1, 3)
    q_x = l2norm(q_x) * f64(qx_scale)
    q_a = l2norm(q_a) * f64(qa_scale)
    q = np.concatenate([q_x, q_a], axis=-1)
    cos, sin = rope_tables()
    return q * cos + rotate_half(q) * sin

@@ -1,0 +1,348 @@
+from contextlib import ExitStack
+
+import concourse.mybir as mybir
+from concourse.masks import make_identity
+
+B, N, D, H, DH = 4, 640, 1024, 16, 64
+P = 128
+FLOPS = 2 * 2 * B * N * D * H * DH
+
+F32 = mybir.dt.float32
+BF16 = mybir.dt.bfloat16
+I32 = mybir.dt.int32
+U32 = mybir.dt.uint32
+U8 = mybir.dt.uint8
+E5X4 = mybir.dt.float8_e5m2_x4
+ACT = mybir.ActivationFunctionType
+ALU = mybir.AluOpType
+
+PI = 3.141592653589793
+RATIO = 10000.0 ** (-1.0 / DH)
+EPS2 = 1e-24
+T_TILES = N // P
+TILES = B * T_TILES
+HALF = 512
+HEADS = HALF // DH
+
+
+def tile_cmattention_pa_kernel(tc, x, a, Wq_x, Wq_a, qx_scale, qa_scale, out):
+    nc = tc.nc
+    acts = (x, a)
+    weights = (Wq_x, Wq_a)
+    gains = (qx_scale, qa_scale)
+
+    with ExitStack() as ctx:
+        const = ctx.enter_context(tc.tile_pool(name="const", bufs=1))
+        stream = ctx.enter_context(tc.tile_pool(name="stream", bufs=1))
+        psum = ctx.enter_context(tc.psum_pool(name="psum", bufs=1))
+
+        raw_tiles = {}
+        wraw_tiles = {}
+        code_tiles = {}
+        unit_tiles = {}
+
+        def load_tokens(i):
+            t, b = divmod(i, B)
+            raw = stream.tile([P, 2, D], BF16, name="raw", tag="raw", bufs=4)
+            for s in (0, 1):
+                nc.sync.dma_start(out=raw[:, s, :], in_=acts[s][b, t * P : (t + 1) * P, :])
+            raw_tiles[i] = raw
+
+        def load_weights(s, piece):
+            wr = stream.tile([P, 2, D], BF16, name="wr", tag="wr", bufs=8)
+            nc.sync.dma_start(
+                out=wr[:],
+                in_=weights[s][piece * 256 : (piece + 1) * 256, :].rearrange("(c p) k -> p c k", p=P),
+            )
+            wraw_tiles[(s, piece)] = wr
+
+        load_tokens(0)
+        load_weights(0, 0)
+        load_weights(0, 1)
+        load_weights(1, 0)
+        load_weights(1, 1)
+        load_tokens(1)
+        load_weights(0, 2)
+        load_weights(0, 3)
+        load_weights(1, 2)
+        load_weights(1, 3)
+        load_tokens(2)
+        load_tokens(3)
+
+        ident_f = const.tile([P, P], F32, name="ident_f", tag="ident_f")
+        make_identity(nc, ident_f[:])
+        ident_b = const.tile([P, P], BF16, name="ident_b", tag="ident_b")
+        make_identity(nc, ident_b[:])
+
+        one = const.tile([P, 1], F32, name="one", tag="one")
+        nc.vector.memset(one[:], 1.0)
+        pos_eps2 = const.tile([P, 1], F32, name="pos_eps2", tag="pos_eps2")
+        nc.vector.memset(pos_eps2[:], EPS2)
+        neg_eps2 = const.tile([P, 1], F32, name="neg_eps2", tag="neg_eps2")
+        nc.vector.memset(neg_eps2[:], -EPS2)
+        warm = const.tile([P, 1], F32, name="warm", tag="warm")
+        nc.scalar.activation(out=warm[:], in_=one[:], func=ACT.Sin)
+        junk = const.tile([P, DH], F32, name="junk", tag="junk")
+
+        wcodes = []
+        wscales = []
+        for s in (0, 1):
+            wc = const.tile([P, 2, H * DH], U32, name="wc%d" % s, tag="wc%d" % s, align_bytes=64)
+            ws = const.tile([P, 2, H * DH], U8, name="ws%d" % s, tag="ws%d" % s, align_bytes=64)
+            wcodes.append(wc)
+            wscales.append(ws)
+
+        frow = const.tile([P, P], F32, name="frow", tag="frow")
+        nc.vector.memset(frow[:, 0:1], 1.0)
+        for m in (1, 2, 4, 8, 16, 32):
+            nc.vector.tensor_scalar(
+                out=frow[:, m : 2 * m], in0=frow[:, 0:m], scalar1=RATIO**m, scalar2=None, op0=ALU.mult
+            )
+        nc.vector.tensor_copy(out=frow[:, DH : 2 * DH], in_=frow[:, 0:DH])
+        fps = psum.tile([P, P], F32, name="fps", tag="tp", bufs=2)
+        nc.tensor.transpose(fps[:], frow[:], ident_f[:])
+        turns = const.tile([P, 1], F32, name="turns", tag="turns")
+        nc.vector.tensor_scalar(
+            out=turns[:], in0=fps[:, 0:1], scalar1=1.0 / (2.0 * PI), scalar2=None, op0=ALU.mult
+        )
+
+        NB = P + T_TILES - 1
+        nb = const.tile([P, NB], F32, name="nb", tag="nb")
+        nc.gpsimd.iota(
+            nb[:, 0:P], pattern=[[1, P]], base=0, channel_multiplier=0, allow_small_or_imprecise_dtypes=True
+        )
+        nc.gpsimd.iota(
+            nb[:, P:NB],
+            pattern=[[P, T_TILES - 1]],
+            base=P,
+            channel_multiplier=0,
+            allow_small_or_imprecise_dtypes=True,
+        )
+        y = const.tile([P, 2, NB], F32, name="y", tag="y")
+        nc.vector.tensor_scalar(out=y[:, 0, :], in0=nb[:], scalar1=turns[:, 0:1], scalar2=None, op0=ALU.mult)
+        nc.vector.tensor_scalar(
+            out=y[:, 1, :], in0=nb[:], scalar1=turns[:, 0:1], scalar2=0.75, op0=ALU.mult, op1=ALU.add
+        )
+        ki = const.tile([P, 2, NB], I32, name="ki", tag="ki")
+        nc.vector.tensor_copy(out=ki[:], in_=y[:])
+        kf = const.tile([P, 2, NB], F32, name="kf", tag="kf")
+        nc.vector.tensor_copy(out=kf[:], in_=ki[:])
+        frac = const.tile([P, 2, NB], F32, name="frac", tag="frac")
+        nc.vector.tensor_tensor(out=frac[:], in0=y[:], in1=kf[:], op=ALU.subtract)
+        half_sin = const.tile([P, 2, NB], F32, name="half_sin", tag="half_sin")
+        nc.scalar.activation(out=half_sin[:], in_=frac[:], func=ACT.Sin, scale=PI)
+        sq = const.tile([P, 2, NB], F32, name="sq", tag="sq")
+        nc.scalar.activation(out=sq[:], in_=half_sin[:], func=ACT.Square)
+        nc.scalar.activation(out=warm[:], in_=sq[:, 0, 0:1], func=ACT.Sqrt, bias=one[:, 0:1])
+
+        trig = const.tile([P, 2, N], F32, name="trig", tag="trig")
+        nc.vector.tensor_scalar(
+            out=trig[:, :, 0:P], in0=sq[:, :, 0:P], scalar1=-2.0, scalar2=1.0, op0=ALU.mult, op1=ALU.add
+        )
+        step = const.tile([P, 2, T_TILES - 1], F32, name="step", tag="step")
+        nc.vector.tensor_scalar(
+            out=step[:], in0=sq[:, :, P:NB], scalar1=-2.0, scalar2=1.0, op0=ALU.mult, op1=ALU.add
+        )
+        split = const.tile([P, 2, N], BF16, name="split", tag="split")
+
+        def split_columns(lo, hi):
+            nc.vector.tensor_copy(out=split[:, :, lo:hi], in_=trig[:, :, lo:hi])
+            nc.vector.tensor_tensor(
+                out=split[DH:P, :, lo:hi], in0=trig[DH:P, :, lo:hi], in1=split[DH:P, :, lo:hi], op=ALU.subtract
+            )
+
+        split_columns(0, P)
+
+        gpad = const.tile([P, P], BF16, name="gpad", tag="gpad")
+        nc.gpsimd.memset(gpad[:], 0.0)
+        for s in (0, 1):
+            rows = gains[s].rearrange("h o d -> h (o d)")
+            for i in (0, 1):
+                nc.scalar.dma_start(out=gpad[H * s : H * (s + 1), DH * i : DH * (i + 1)], in_=rows)
+        gps = psum.tile([P, P], BF16, name="gps", tag="tp", bufs=2)
+        nc.tensor.transpose(gps[:], gpad[:], ident_b[:])
+        gcol = const.tile([P, 2 * H], BF16, name="gcol", tag="gcol")
+        nc.vector.tensor_copy(out=gcol[:], in_=gps[:, 0 : 2 * H])
+        eye2 = const.tile([P, DH], BF16, name="eye2", tag="eye2")
+        nc.gpsimd.tensor_tensor(out=eye2[:], in0=ident_b[:, 0:DH], in1=ident_b[:, DH:P], op=ALU.add)
+        diag = []
+        for s in (0, 1):
+            dm = const.tile([P, H, DH], BF16, name="dm%d" % s, tag="dm%d" % s)
+            nc.vector.tensor_tensor(
+                out=dm[:],
+                in0=eye2[:].unsqueeze(1).to_broadcast([P, H, DH]),
+                in1=gcol[:, H * s : H * (s + 1)].unsqueeze(2).to_broadcast([P, H, DH]),
+                op=ALU.mult,
+            )
+            diag.append(dm)
+
+        tables = []
+        for t in range(T_TILES):
+            tx = const.tile([P, H, 2, DH], F32, name="tx%d" % t, tag="tx%d" % t)
+            ty = const.tile([P, H, 2, DH], F32, name="ty%d" % t, tag="ty%d" % t)
+            tables.append((tx, ty))
+
+        parts = ((0, 0, 0, 1.0), (1, 0, 1, 1.0), (1, 1, 0, -1.0), (0, 1, 1, 1.0))
+
+        def table_piece(t, e):
+            kind, s, q, sign = parts[e // 2]
+            h0 = HEADS * (e % 2)
+            ps = psum.tile([P, HALF], F32, name="tps", tag="tp", bufs=2)
+            nc.tensor.matmul(
+                out=ps[:],
+                lhsT=split[:, kind, t * P : (t + 1) * P],
+                rhs=diag[s][:, h0 : h0 + HEADS, :].rearrange("p h j -> p (h j)"),
+                start=True,
+                stop=True,
+            )
+            nc.scalar.activation(
+                out=tables[t][s][:, h0 : h0 + HEADS, q, :],
+                in_=ps[:].rearrange("p (h j) -> p h j", j=DH),
+                func=ACT.Copy,
+                scale=sign,
+            )
+
+        def prep_tokens(i):
+            raw = raw_tiles[i]
+            words = raw[:].rearrange("p s k -> p (s k)").bitcast(F32)
+            grouped = stream.tile([P, 2 * D], BF16, name="grouped", tag="grouped", bufs=3, align_bytes=64)
+            gwords = grouped[:].bitcast(F32).rearrange("p (s g r u) -> p s g r u", s=2, g=2, u=2)
+            for s in (0, 1):
+                bank = psum.tile([P, 2, 2, P], F32, name="bank", tag="tp", bufs=2)
+                for g in (0, 1):
+                    for u in (0, 1):
+                        lo = 512 * s + 256 * g
+                        nc.tensor.transpose(bank[:, g, u, :], words[:, lo + u : lo + 256 : 2], ident_f[:])
+                nc.scalar.copy(out=gwords[:, s], in_=bank[:].rearrange("p g u r -> p g r u"))
+            codes = stream.tile([P, 4 * P], U32, name="codes", tag="codes", bufs=4, align_bytes=64)
+            scales = stream.tile([P, 4 * P], U8, name="scales", tag="scales", bufs=4, align_bytes=64)
+            nc.vector.quantize_mx(out=codes[:].bitcast(E5X4), scales=scales[:], in_=grouped[:])
+            code_tiles[i] = (codes, scales)
+
+        def prep_weights(s, piece):
+            wr = wraw_tiles[(s, piece)]
+            words = wr[:].rearrange("p c k -> p (c k)").bitcast(F32)
+            cols = slice(256 * piece, 256 * (piece + 1))
+            for g in (0, 1):
+                bank = psum.tile([P, 2, 2, P], F32, name="wbank", tag="tp", bufs=2)
+                for c in (0, 1):
+                    for u in (0, 1):
+                        lo = 512 * c + 256 * g
+                        nc.tensor.transpose(bank[:, c, u, :], words[:, lo + u : lo + 256 : 2], ident_f[:])
+                wg = stream.tile([P, D], BF16, name="wg", tag="wg", bufs=3, align_bytes=64)
+                nc.scalar.copy(
+                    out=wg[:].bitcast(F32).rearrange("p (c r u) -> p c r u", c=2, u=2),
+                    in_=bank[:].rearrange("p c u r -> p c r u"),
+                )
+                nc.vector.quantize_mx(
+                    out=wcodes[s][:, g, cols].bitcast(E5X4), scales=wscales[s][:, g, cols], in_=wg[:]
+                )
+
+        def project(unit):
+            i, c = unit
+            codes, scales = code_tiles[i]
+            wcols = slice(HALF * c, HALF * (c + 1))
+            acc = []
+            for s in (0, 1):
+                bank = psum.tile([P, HALF], F32, name="acc%d" % s, tag="acc%d" % s, bufs=3)
+                for g in (0, 1):
+                    cols = slice((2 * s + g) * P, (2 * s + g + 1) * P)
+                    nc.tensor.matmul_mx(
+                        out=bank[:],
+                        lhsT=codes[:, cols].bitcast(E5X4),
+                        lhsT_scale=scales[:, cols],
+                        rhs=wcodes[s][:, g, wcols].bitcast(E5X4),
+                        rhs_scale=wscales[s][:, g, wcols],
+                        start=(g == 0),
+                        stop=(g == 1),
+                    )
+                acc.append(bank)
+            ss = stream.tile([P, 2 * HEADS], F32, name="ss", tag="ss", bufs=4)
+            for s in (0, 1):
+                for hh in range(HEADS):
+                    nc.scalar.activation(
+                        out=junk[:],
+                        in_=acc[s][:, DH * hh : DH * (hh + 1)],
+                        func=ACT.Square,
+                        accum_out=ss[:, HEADS * s + hh : HEADS * s + hh + 1],
+                    )
+            floor = stream.tile([P, 2 * HEADS], F32, name="floor", tag="floor", bufs=4)
+            nc.scalar.activation(out=floor[:], in_=ss[:], func=ACT.Relu, bias=neg_eps2[:, 0:1])
+            norm = stream.tile([P, 2 * HEADS], F32, name="norm", tag="norm", bufs=4)
+            nc.scalar.activation(out=norm[:], in_=floor[:], func=ACT.Sqrt, bias=pos_eps2[:, 0:1])
+            inv = stream.tile([P, 2 * HEADS], F32, name="inv", tag="inv", bufs=4)
+            nc.vector.reciprocal(out=inv[:], in_=norm[:])
+            unit_tiles[unit] = (acc, inv)
+
+        def rotate(unit):
+            i, c = unit
+            t, b = divmod(i, B)
+            acc, inv = unit_tiles[unit]
+            xp = stream.tile([P, HEADS, 2 * DH], F32, name="xp", tag="xp", bufs=4)
+            yp = stream.tile([P, HEADS, 2 * DH], F32, name="yp", tag="yp", bufs=3)
+            prod = (xp, yp)
+            for hh in range(HEADS):
+                for s in (0, 1):
+                    nc.vector.scalar_tensor_tensor(
+                        out=prod[s][:, hh, :].rearrange("p (q j) -> p q j", q=2),
+                        in0=acc[s][:, DH * hh : DH * (hh + 1)].unsqueeze(1).to_broadcast([P, 2, DH]),
+                        scalar=inv[:, HEADS * s + hh : HEADS * s + hh + 1],
+                        in1=tables[t][s][:, HEADS * c + hh, :, :],
+                        op0=ALU.mult,
+                        op1=ALU.mult,
+                    )
+                if hh % 4 == 3:
+                    hs = slice(hh - 3, hh + 1)
+                    nc.gpsimd.tensor_tensor(out=xp[:, hs, :], in0=xp[:, hs, :], in1=yp[:, hs, :], op=ALU.add)
+            nc.sync.dma_start(
+                out=out[b, HEADS * c : HEADS * (c + 1), t * P : (t + 1) * P, :].rearrange("h n d -> n h d"),
+                in_=xp[:],
+            )
+
+        prep_tokens(0)
+        for s in (0, 1):
+            for piece in (0, 1):
+                prep_weights(s, piece)
+        prep_tokens(1)
+        for e in range(8):
+            table_piece(0, e)
+
+        for t in range(1, T_TILES):
+            cols = slice(t * P, (t + 1) * P)
+            cstep = step[:, 0, t - 1 : t]
+            sstep = step[:, 1, t - 1 : t]
+            cross = stream.tile([P, 2, P], F32, name="cross", tag="cross", bufs=2)
+            nc.vector.tensor_scalar(
+                out=cross[:, 0, :], in0=trig[:, 1, 0:P], scalar1=sstep, scalar2=None, op0=ALU.mult
+            )
+            nc.vector.tensor_scalar(
+                out=cross[:, 1, :], in0=trig[:, 0, 0:P], scalar1=sstep, scalar2=None, op0=ALU.mult
+            )
+            nc.vector.scalar_tensor_tensor(
+                out=trig[:, 0, cols], in0=trig[:, 0, 0:P], scalar=cstep, in1=cross[:, 0, :],
+                op0=ALU.mult, op1=ALU.subtract,
+            )
+            nc.vector.scalar_tensor_tensor(
+                out=trig[:, 1, cols], in0=trig[:, 1, 0:P], scalar=cstep, in1=cross[:, 1, :],
+                op0=ALU.mult, op1=ALU.add,
+            )
+        split_columns(P, N)
+
+        units = [(0, 0), (1, 0), (0, 1), (1, 1)] + [(i, c) for i in range(2, TILES) for c in (0, 1)]
+        project(units[0])
+        for k in range(len(units)):
+            if k == 0:
+                for s in (0, 1):
+                    for piece in (2, 3):
+                        prep_weights(s, piece)
+            if k % 2 == 0:
+                if k // 2 + 4 < TILES:
+                    load_tokens(k // 2 + 4)
+                if k // 2 + 2 < TILES:
+                    prep_tokens(k // 2 + 2)
+            if k % 8 < 4 and k // 8 + 1 < T_TILES:
+                table_piece(k // 8 + 1, 2 * (k % 8))
+                table_piece(k // 8 + 1, 2 * (k % 8) + 1)
+            if k + 1 < len(units):
+                project(units[k + 1])
+            rotate(units[k])

@@ -82,7 +82,6 @@ def tile_cmattention_pa_kernel(tc, x, a, Wq_x, Wq_a, qx_scale, qa_scale, out):
         nc.vector.memset(neg_eps2[:], -EPS2)
         warm = const.tile([P, 1], F32, name="warm", tag="warm")
         nc.scalar.activation(out=warm[:], in_=one[:], func=ACT.Sin)
-        junk = const.tile([P, DH], F32, name="junk", tag="junk")
 
         wcodes = []
         wscales = []
@@ -195,12 +194,21 @@ def tile_cmattention_pa_kernel(tc, x, a, Wq_x, Wq_a, qx_scale, qa_scale, out):
                 start=True,
                 stop=True,
             )
-            nc.scalar.activation(
-                out=tables[t][s][:, h0 : h0 + HEADS, q, :],
-                in_=ps[:].rearrange("p (h j) -> p h j", j=DH),
-                func=ACT.Copy,
-                scale=sign,
-            )
+            if t == 0:
+                nc.vector.tensor_scalar(
+                    out=tables[t][s][:, h0 : h0 + HEADS, q, :],
+                    in0=ps[:].rearrange("p (h j) -> p h j", j=DH),
+                    scalar1=sign,
+                    scalar2=None,
+                    op0=ALU.mult,
+                )
+            else:
+                nc.scalar.activation(
+                    out=tables[t][s][:, h0 : h0 + HEADS, q, :],
+                    in_=ps[:].rearrange("p (h j) -> p h j", j=DH),
+                    func=ACT.Copy,
+                    scale=sign,
+                )
 
         def prep_tokens(i):
             raw = raw_tiles[i]
@@ -258,10 +266,11 @@ def tile_cmattention_pa_kernel(tc, x, a, Wq_x, Wq_a, qx_scale, qa_scale, out):
                     )
                 acc.append(bank)
             ss = stream.tile([P, 2 * HEADS], F32, name="ss", tag="ss", bufs=4)
+            junk = stream.tile([P, 2 * HEADS, DH], F32, name="junk", tag="junk", bufs=2)
             for s in (0, 1):
                 for hh in range(HEADS):
                     nc.scalar.activation(
-                        out=junk[:],
+                        out=junk[:, HEADS * s + hh, :],
                         in_=acc[s][:, DH * hh : DH * (hh + 1)],
                         func=ACT.Square,
                         accum_out=ss[:, HEADS * s + hh : HEADS * s + hh + 1],

@@ -23,6 +23,7 @@ T_TILES = N // P
 TILES = B * T_TILES
 HALF = 512
 HEADS = HALF // DH
+PLAIN_FILLERS = 18
 
 
 def tile_cmattention_pa_kernel(tc, x, a, Wq_x, Wq_a, qx_scale, qa_scale, out):
@@ -80,6 +81,8 @@ def tile_cmattention_pa_kernel(tc, x, a, Wq_x, Wq_a, qx_scale, qa_scale, out):
         nc.vector.memset(pos_eps2[:], EPS2)
         neg_eps2 = const.tile([P, 1], F32, name="neg_eps2", tag="neg_eps2")
         nc.vector.memset(neg_eps2[:], -EPS2)
+        zeros = const.tile([P, HALF], BF16, name="zeros", tag="zeros")
+        nc.vector.memset(zeros[:], 0.0)
         warm = const.tile([P, 1], F32, name="warm", tag="warm")
         nc.scalar.activation(out=warm[:], in_=one[:], func=ACT.Sin)
 
@@ -90,6 +93,11 @@ def tile_cmattention_pa_kernel(tc, x, a, Wq_x, Wq_a, qx_scale, qa_scale, out):
             ws = const.tile([P, 2, H * DH], U8, name="ws%d" % s, tag="ws%d" % s, align_bytes=64)
             wcodes.append(wc)
             wscales.append(ws)
+
+        WARM = 6
+        warm_bank = psum.tile([P, HALF], F32, name="warm_bank", tag="tp", bufs=2)
+        for w in range(WARM):
+            nc.tensor.matmul(out=warm_bank[:], lhsT=zeros[:, 0:P], rhs=zeros[:], start=True, stop=True)
 
         frow = const.tile([P, P], F32, name="frow", tag="frow")
         nc.vector.memset(frow[:, 0:1], 1.0)
@@ -194,7 +202,7 @@ def tile_cmattention_pa_kernel(tc, x, a, Wq_x, Wq_a, qx_scale, qa_scale, out):
                 start=True,
                 stop=True,
             )
-            if t == 0:
+            if t == 0 and e % 2 == 0:
                 nc.vector.tensor_scalar(
                     out=tables[t][s][:, h0 : h0 + HEADS, q, :],
                     in0=ps[:].rearrange("p (h j) -> p h j", j=DH),
@@ -210,21 +218,46 @@ def tile_cmattention_pa_kernel(tc, x, a, Wq_x, Wq_a, qx_scale, qa_scale, out):
                     scale=sign,
                 )
 
-        def prep_tokens(i):
+        fill_count = [WARM]
+
+        def filler(bank2d):
+            if fill_count[0] < PLAIN_FILLERS:
+                nc.tensor.matmul(out=bank2d, lhsT=zeros[:, 0:P], rhs=zeros[:], start=True, stop=True)
+            else:
+                nc.tensor.matmul_mx(
+                    out=bank2d,
+                    lhsT=wcodes[0][:, 0, 0:P].bitcast(E5X4),
+                    lhsT_scale=wscales[0][:, 0, 0:P],
+                    rhs=wcodes[0][:, 0, 0:HALF].bitcast(E5X4),
+                    rhs_scale=wscales[0][:, 0, 0:HALF],
+                    start=True,
+                    stop=True,
+                )
+            fill_count[0] += 1
+
+        group_tiles = {}
+
+        def turn_tokens(j):
+            i, s = divmod(j, 2)
             raw = raw_tiles[i]
             words = raw[:].rearrange("p s k -> p (s k)").bitcast(F32)
-            grouped = stream.tile([P, 2 * D], BF16, name="grouped", tag="grouped", bufs=3, align_bytes=64)
+            if s == 0:
+                grouped = stream.tile([P, 2 * D], BF16, name="grouped", tag="grouped", bufs=3, align_bytes=64)
+                group_tiles[i] = grouped
+            grouped = group_tiles[i]
             gwords = grouped[:].bitcast(F32).rearrange("p (s g r u) -> p s g r u", s=2, g=2, u=2)
-            for s in (0, 1):
-                bank = psum.tile([P, 2, 2, P], F32, name="bank", tag="tp", bufs=2)
-                for g in (0, 1):
-                    for u in (0, 1):
-                        lo = 512 * s + 256 * g
-                        nc.tensor.transpose(bank[:, g, u, :], words[:, lo + u : lo + 256 : 2], ident_f[:])
-                nc.scalar.copy(out=gwords[:, s], in_=bank[:].rearrange("p g u r -> p g r u"))
+            bank = psum.tile([P, 2, 2, P], F32, name="bank", tag="tp", bufs=2)
+            filler(bank[:].rearrange("p g u r -> p (g u r)"))
+            for g in (0, 1):
+                for u in (0, 1):
+                    lo = 512 * s + 256 * g
+                    nc.tensor.transpose(bank[:, g, u, :], words[:, lo + u : lo + 256 : 2], ident_f[:])
+            nc.scalar.copy(out=gwords[:, s], in_=bank[:].rearrange("p g u r -> p g r u"))
+
+        def quantise_tokens(i):
             codes = stream.tile([P, 4 * P], U32, name="codes", tag="codes", bufs=4, align_bytes=64)
             scales = stream.tile([P, 4 * P], U8, name="scales", tag="scales", bufs=4, align_bytes=64)
-            nc.vector.quantize_mx(out=codes[:].bitcast(E5X4), scales=scales[:], in_=grouped[:])
+            nc.vector.quantize_mx(out=codes[:].bitcast(E5X4), scales=scales[:], in_=group_tiles[i][:])
             code_tiles[i] = (codes, scales)
 
         def prep_weights(s, piece):
@@ -233,6 +266,7 @@ def tile_cmattention_pa_kernel(tc, x, a, Wq_x, Wq_a, qx_scale, qa_scale, out):
             cols = slice(256 * piece, 256 * (piece + 1))
             for g in (0, 1):
                 bank = psum.tile([P, 2, 2, P], F32, name="wbank", tag="tp", bufs=2)
+                filler(bank[:].rearrange("p c u r -> p (c u r)"))
                 for c in (0, 1):
                     for u in (0, 1):
                         lo = 512 * c + 256 * g
@@ -246,77 +280,81 @@ def tile_cmattention_pa_kernel(tc, x, a, Wq_x, Wq_a, qx_scale, qa_scale, out):
                     out=wcodes[s][:, g, cols].bitcast(E5X4), scales=wscales[s][:, g, cols], in_=wg[:]
                 )
 
-        def project(unit):
-            i, c = unit
+        units = [(0, 0), (1, 0), (0, 1), (1, 1)] + [(i, c) for i in range(2, TILES) for c in (0, 1)]
+        acc_tiles = {}
+        sum_tiles = {}
+        inv_tiles = {}
+        prod_tiles = {}
+
+        def project(k, s):
+            i, c = units[k]
             codes, scales = code_tiles[i]
             wcols = slice(HALF * c, HALF * (c + 1))
-            acc = []
-            for s in (0, 1):
-                bank = psum.tile([P, HALF], F32, name="acc%d" % s, tag="acc%d" % s, bufs=3)
-                for g in (0, 1):
-                    cols = slice((2 * s + g) * P, (2 * s + g + 1) * P)
-                    nc.tensor.matmul_mx(
-                        out=bank[:],
-                        lhsT=codes[:, cols].bitcast(E5X4),
-                        lhsT_scale=scales[:, cols],
-                        rhs=wcodes[s][:, g, wcols].bitcast(E5X4),
-                        rhs_scale=wscales[s][:, g, wcols],
-                        start=(g == 0),
-                        stop=(g == 1),
-                    )
-                acc.append(bank)
-            ss = stream.tile([P, 2 * HEADS], F32, name="ss", tag="ss", bufs=4)
-            junk = stream.tile([P, 2 * HEADS, DH], F32, name="junk", tag="junk", bufs=2)
-            for s in (0, 1):
-                for hh in range(HEADS):
-                    nc.scalar.activation(
-                        out=junk[:, HEADS * s + hh, :],
-                        in_=acc[s][:, DH * hh : DH * (hh + 1)],
-                        func=ACT.Square,
-                        accum_out=ss[:, HEADS * s + hh : HEADS * s + hh + 1],
-                    )
-            floor = stream.tile([P, 2 * HEADS], F32, name="floor", tag="floor", bufs=4)
-            nc.scalar.activation(out=floor[:], in_=ss[:], func=ACT.Relu, bias=neg_eps2[:, 0:1])
-            norm = stream.tile([P, 2 * HEADS], F32, name="norm", tag="norm", bufs=4)
-            nc.scalar.activation(out=norm[:], in_=floor[:], func=ACT.Sqrt, bias=pos_eps2[:, 0:1])
-            inv = stream.tile([P, 2 * HEADS], F32, name="inv", tag="inv", bufs=4)
-            nc.vector.reciprocal(out=inv[:], in_=norm[:])
-            unit_tiles[unit] = (acc, inv)
-
-        def rotate(unit):
-            i, c = unit
-            t, b = divmod(i, B)
-            acc, inv = unit_tiles[unit]
-            xp = stream.tile([P, HEADS, 2 * DH], F32, name="xp", tag="xp", bufs=4)
-            yp = stream.tile([P, HEADS, 2 * DH], F32, name="yp", tag="yp", bufs=3)
-            prod = (xp, yp)
+            bank = psum.tile([P, HALF], F32, name="acc%d" % s, tag="acc%d" % s, bufs=3)
+            for g in (0, 1):
+                cols = slice((2 * s + g) * P, (2 * s + g + 1) * P)
+                nc.tensor.matmul_mx(
+                    out=bank[:],
+                    lhsT=codes[:, cols].bitcast(E5X4),
+                    lhsT_scale=scales[:, cols],
+                    rhs=wcodes[s][:, g, wcols].bitcast(E5X4),
+                    rhs_scale=wscales[s][:, g, wcols],
+                    start=(g == 0),
+                    stop=(g == 1),
+                )
+            acc_tiles[(k, s)] = bank
+            if s == 0:
+                ss = stream.tile([P, 2 * HEADS], F32, name="ss", tag="ss", bufs=5)
+                junk = stream.tile([P, 2 * HEADS, DH], F32, name="junk", tag="junk", bufs=2)
+                sum_tiles[k] = (ss, junk)
+            ss, junk = sum_tiles[k]
             for hh in range(HEADS):
-                for s in (0, 1):
-                    nc.vector.scalar_tensor_tensor(
-                        out=prod[s][:, hh, :].rearrange("p (q j) -> p q j", q=2),
-                        in0=acc[s][:, DH * hh : DH * (hh + 1)].unsqueeze(1).to_broadcast([P, 2, DH]),
-                        scalar=inv[:, HEADS * s + hh : HEADS * s + hh + 1],
-                        in1=tables[t][s][:, HEADS * c + hh, :, :],
-                        op0=ALU.mult,
-                        op1=ALU.mult,
-                    )
-                if hh % 4 == 3:
+                nc.scalar.activation(
+                    out=junk[:, HEADS * s + hh, :],
+                    in_=bank[:, DH * hh : DH * (hh + 1)],
+                    func=ACT.Square,
+                    accum_out=ss[:, HEADS * s + hh : HEADS * s + hh + 1],
+                )
+
+        def norms(k):
+            ss = sum_tiles[k][0]
+            floor = stream.tile([P, 2 * HEADS], F32, name="floor", tag="floor", bufs=2)
+            nc.scalar.activation(out=floor[:], in_=ss[:], func=ACT.Relu, bias=neg_eps2[:, 0:1])
+            norm = stream.tile([P, 2 * HEADS], F32, name="norm", tag="norm", bufs=2)
+            nc.scalar.activation(out=norm[:], in_=floor[:], func=ACT.Sqrt, bias=pos_eps2[:, 0:1])
+            inv = stream.tile([P, 2 * HEADS], F32, name="inv", tag="inv", bufs=5)
+            nc.vector.reciprocal(out=inv[:], in_=norm[:])
+            inv_tiles[k] = inv
+
+        def rotate(k, s):
+            i, c = units[k]
+            t, b = divmod(i, B)
+            bank = acc_tiles[(k, s)]
+            inv = inv_tiles[k]
+            if s == 0:
+                xp = stream.tile([P, HEADS, 2 * DH], F32, name="xp", tag="xp", bufs=4)
+                yp = stream.tile([P, HEADS, 2 * DH], F32, name="yp", tag="yp", bufs=3)
+                prod_tiles[k] = (xp, yp)
+            xp, yp = prod_tiles[k]
+            for hh in range(HEADS):
+                nc.vector.scalar_tensor_tensor(
+                    out=prod_tiles[k][s][:, hh, :].rearrange("p (q j) -> p q j", q=2),
+                    in0=bank[:, DH * hh : DH * (hh + 1)].unsqueeze(1).to_broadcast([P, 2, DH]),
+                    scalar=inv[:, HEADS * s + hh : HEADS * s + hh + 1],
+                    in1=tables[t][s][:, HEADS * c + hh, :, :],
+                    op0=ALU.mult,
+                    op1=ALU.mult,
+                )
+                if s == 1 and hh % 4 == 3:
                     hs = slice(hh - 3, hh + 1)
                     nc.gpsimd.tensor_tensor(out=xp[:, hs, :], in0=xp[:, hs, :], in1=yp[:, hs, :], op=ALU.add)
-            nc.sync.dma_start(
-                out=out[b, HEADS * c : HEADS * (c + 1), t * P : (t + 1) * P, :].rearrange("h n d -> n h d"),
-                in_=xp[:],
-            )
+            if s == 1:
+                nc.sync.dma_start(
+                    out=out[b, HEADS * c : HEADS * (c + 1), t * P : (t + 1) * P, :].rearrange("h n d -> n h d"),
+                    in_=xp[:],
+                )
 
-        prep_tokens(0)
-        for s in (0, 1):
-            for piece in (0, 1):
-                prep_weights(s, piece)
-        prep_tokens(1)
-        for e in range(8):
-            table_piece(0, e)
-
-        for t in range(1, T_TILES):
+        def later_angles(t):
             cols = slice(t * P, (t + 1) * P)
             cstep = step[:, 0, t - 1 : t]
             sstep = step[:, 1, t - 1 : t]
@@ -335,23 +373,57 @@ def tile_cmattention_pa_kernel(tc, x, a, Wq_x, Wq_a, qx_scale, qa_scale, out):
                 out=trig[:, 1, cols], in0=trig[:, 1, 0:P], scalar=cstep, in1=cross[:, 1, :],
                 op0=ALU.mult, op1=ALU.add,
             )
-        split_columns(P, N)
+            split_columns(t * P, (t + 1) * P)
 
-        units = [(0, 0), (1, 0), (0, 1), (1, 1)] + [(i, c) for i in range(2, TILES) for c in (0, 1)]
-        project(units[0])
-        for k in range(len(units)):
-            if k == 0:
-                for s in (0, 1):
-                    for piece in (2, 3):
-                        prep_weights(s, piece)
-            if k % 2 == 0:
-                if k // 2 + 4 < TILES:
-                    load_tokens(k // 2 + 4)
-                if k // 2 + 2 < TILES:
-                    prep_tokens(k // 2 + 2)
-            if k % 8 < 4 and k // 8 + 1 < T_TILES:
-                table_piece(k // 8 + 1, 2 * (k % 8))
-                table_piece(k // 8 + 1, 2 * (k % 8) + 1)
-            if k + 1 < len(units):
-                project(units[k + 1])
-            rotate(units[k])
+        def later_table(m):
+            table_piece(1 + m // 8, m % 8)
+
+        turn_tokens(0)
+        turn_tokens(1)
+        quantise_tokens(0)
+        load_tokens(4)
+        for s in (0, 1):
+            for piece in (0, 1):
+                prep_weights(s, piece)
+        turn_tokens(2)
+        turn_tokens(3)
+        quantise_tokens(1)
+        load_tokens(5)
+        for e in range(8):
+            table_piece(0, e)
+        for k in (0, 1):
+            project(k, 0)
+            project(k, 1)
+            norms(k)
+        for s in (0, 1):
+            for piece in (2, 3):
+                prep_weights(s, piece)
+        turn_tokens(4)
+        turn_tokens(5)
+        quantise_tokens(2)
+        later_angles(1)
+        later_table(0)
+        later_table(1)
+        project(2, 0)
+        project(2, 1)
+        norms(2)
+
+        n_units = len(units)
+        for k in range(n_units):
+            rotate(k, 0)
+            if k % 2 == 0 and k // 2 + 6 < TILES:
+                load_tokens(k // 2 + 6)
+            if k + 6 < 2 * TILES:
+                turn_tokens(k + 6)
+            if k % 2 == 0 and 3 <= k // 2 + 2 < TILES:
+                quantise_tokens(k // 2 + 2)
+            if k % 8 == 4 and k // 8 + 2 < T_TILES:
+                later_angles(k // 8 + 2)
+            if k + 2 < 8 * (T_TILES - 1):
+                later_table(k + 2)
+            if k + 3 < n_units:
+                project(k + 3, 0)
+            rotate(k, 1)
+            if k + 3 < n_units:
+                project(k + 3, 1)
+                norms(k + 3)

@@ -23,7 +23,6 @@ T_TILES = N // P
 TILES = B * T_TILES
 HALF = 512
 HEADS = HALF // DH
-PLAIN_FILLERS = 18
 
 
 def tile_cmattention_pa_kernel(tc, x, a, Wq_x, Wq_a, qx_scale, qa_scale, out):
@@ -81,8 +80,6 @@ def tile_cmattention_pa_kernel(tc, x, a, Wq_x, Wq_a, qx_scale, qa_scale, out):
         nc.vector.memset(pos_eps2[:], EPS2)
         neg_eps2 = const.tile([P, 1], F32, name="neg_eps2", tag="neg_eps2")
         nc.vector.memset(neg_eps2[:], -EPS2)
-        zeros = const.tile([P, HALF], BF16, name="zeros", tag="zeros")
-        nc.vector.memset(zeros[:], 0.0)
         warm = const.tile([P, 1], F32, name="warm", tag="warm")
         nc.scalar.activation(out=warm[:], in_=one[:], func=ACT.Sin)
 
@@ -93,11 +90,6 @@ def tile_cmattention_pa_kernel(tc, x, a, Wq_x, Wq_a, qx_scale, qa_scale, out):
             ws = const.tile([P, 2, H * DH], U8, name="ws%d" % s, tag="ws%d" % s, align_bytes=64)
             wcodes.append(wc)
             wscales.append(ws)
-
-        WARM = 6
-        warm_bank = psum.tile([P, HALF], F32, name="warm_bank", tag="tp", bufs=2)
-        for w in range(WARM):
-            nc.tensor.matmul(out=warm_bank[:], lhsT=zeros[:, 0:P], rhs=zeros[:], start=True, stop=True)
 
         frow = const.tile([P, P], F32, name="frow", tag="frow")
         nc.vector.memset(frow[:, 0:1], 1.0)
@@ -140,7 +132,7 @@ def tile_cmattention_pa_kernel(tc, x, a, Wq_x, Wq_a, qx_scale, qa_scale, out):
         nc.scalar.activation(out=half_sin[:], in_=frac[:], func=ACT.Sin, scale=PI)
         sq = const.tile([P, 2, NB], F32, name="sq", tag="sq")
         nc.scalar.activation(out=sq[:], in_=half_sin[:], func=ACT.Square)
-        nc.scalar.activation(out=warm[:], in_=sq[:, 0, 0:1], func=ACT.Sqrt, bias=one[:, 0:1])
+        nc.scalar.activation(out=warm[:], in_=sq[:, 0, 0:1], func=ACT.Abs_reciprocal_sqrt, bias=one[:, 0:1])
 
         trig = const.tile([P, 2, N], F32, name="trig", tag="trig")
         nc.vector.tensor_scalar(
@@ -202,7 +194,7 @@ def tile_cmattention_pa_kernel(tc, x, a, Wq_x, Wq_a, qx_scale, qa_scale, out):
                 start=True,
                 stop=True,
             )
-            if t == 0 and e % 2 == 0:
+            if e % 2 == 0:
                 nc.vector.tensor_scalar(
                     out=tables[t][s][:, h0 : h0 + HEADS, q, :],
                     in0=ps[:].rearrange("p (h j) -> p h j", j=DH),
@@ -218,212 +210,164 @@ def tile_cmattention_pa_kernel(tc, x, a, Wq_x, Wq_a, qx_scale, qa_scale, out):
                     scale=sign,
                 )
 
-        fill_count = [WARM]
-
-        def filler(bank2d):
-            if fill_count[0] < PLAIN_FILLERS:
-                nc.tensor.matmul(out=bank2d, lhsT=zeros[:, 0:P], rhs=zeros[:], start=True, stop=True)
-            else:
-                nc.tensor.matmul_mx(
-                    out=bank2d,
-                    lhsT=wcodes[0][:, 0, 0:P].bitcast(E5X4),
-                    lhsT_scale=wscales[0][:, 0, 0:P],
-                    rhs=wcodes[0][:, 0, 0:HALF].bitcast(E5X4),
-                    rhs_scale=wscales[0][:, 0, 0:HALF],
-                    start=True,
-                    stop=True,
-                )
-            fill_count[0] += 1
-
         group_tiles = {}
 
-        def turn_tokens(j):
-            i, s = divmod(j, 2)
+        def turn_tokens(i):
             raw = raw_tiles[i]
             words = raw[:].rearrange("p s k -> p (s k)").bitcast(F32)
-            if s == 0:
-                grouped = stream.tile([P, 2 * D], BF16, name="grouped", tag="grouped", bufs=3, align_bytes=64)
-                group_tiles[i] = grouped
-            grouped = group_tiles[i]
+            grouped = stream.tile([P, 2 * D], BF16, name="grouped", tag="grouped", bufs=3, align_bytes=64)
             gwords = grouped[:].bitcast(F32).rearrange("p (s g r u) -> p s g r u", s=2, g=2, u=2)
-            bank = psum.tile([P, 2, 2, P], F32, name="bank", tag="tp", bufs=2)
-            filler(bank[:].rearrange("p g u r -> p (g u r)"))
-            for g in (0, 1):
-                for u in (0, 1):
-                    lo = 512 * s + 256 * g
-                    nc.tensor.transpose(bank[:, g, u, :], words[:, lo + u : lo + 256 : 2], ident_f[:])
-            nc.scalar.copy(out=gwords[:, s], in_=bank[:].rearrange("p g u r -> p g r u"))
+            for s in (0, 1):
+                bank = psum.tile([P, 2, 2, P], F32, name="bank", tag="tp", bufs=2)
+                for g in (0, 1):
+                    for u in (0, 1):
+                        lo = 512 * s + 256 * g
+                        nc.tensor.transpose(bank[:, g, u, :], words[:, lo + u : lo + 256 : 2], ident_f[:])
+                nc.scalar.copy(out=gwords[:, s], in_=bank[:].rearrange("p g u r -> p g r u"))
+            group_tiles[i] = grouped
 
         def quantise_tokens(i):
+            grouped = group_tiles[i]
             codes = stream.tile([P, 4 * P], U32, name="codes", tag="codes", bufs=4, align_bytes=64)
             scales = stream.tile([P, 4 * P], U8, name="scales", tag="scales", bufs=4, align_bytes=64)
-            nc.vector.quantize_mx(out=codes[:].bitcast(E5X4), scales=scales[:], in_=group_tiles[i][:])
+            nc.vector.quantize_mx(out=codes[:].bitcast(E5X4), scales=scales[:], in_=grouped[:])
             code_tiles[i] = (codes, scales)
 
-        def prep_weights(s, piece):
+        def prep_weights(s, piece, on_vector):
             wr = wraw_tiles[(s, piece)]
             words = wr[:].rearrange("p c k -> p (c k)").bitcast(F32)
             cols = slice(256 * piece, 256 * (piece + 1))
             for g in (0, 1):
                 bank = psum.tile([P, 2, 2, P], F32, name="wbank", tag="tp", bufs=2)
-                filler(bank[:].rearrange("p c u r -> p (c u r)"))
                 for c in (0, 1):
                     for u in (0, 1):
                         lo = 512 * c + 256 * g
                         nc.tensor.transpose(bank[:, c, u, :], words[:, lo + u : lo + 256 : 2], ident_f[:])
                 wg = stream.tile([P, D], BF16, name="wg", tag="wg", bufs=3, align_bytes=64)
-                nc.scalar.copy(
-                    out=wg[:].bitcast(F32).rearrange("p (c r u) -> p c r u", c=2, u=2),
-                    in_=bank[:].rearrange("p c u r -> p c r u"),
-                )
+                if on_vector and g == 1:
+                    nc.vector.tensor_copy(
+                        out=wg[:].bitcast(F32).rearrange("p (c r u) -> p c r u", c=2, u=2),
+                        in_=bank[:].rearrange("p c u r -> p c r u"),
+                    )
+                else:
+                    nc.scalar.copy(
+                        out=wg[:].bitcast(F32).rearrange("p (c r u) -> p c r u", c=2, u=2),
+                        in_=bank[:].rearrange("p c u r -> p c r u"),
+                    )
                 nc.vector.quantize_mx(
                     out=wcodes[s][:, g, cols].bitcast(E5X4), scales=wscales[s][:, g, cols], in_=wg[:]
                 )
 
-        units = [(0, 0), (1, 0), (0, 1), (1, 1)] + [(i, c) for i in range(2, TILES) for c in (0, 1)]
-        acc_tiles = {}
-        sum_tiles = {}
-        inv_tiles = {}
-        prod_tiles = {}
-
-        def project(k, s):
-            i, c = units[k]
+        def project(unit):
+            i, c = unit
             codes, scales = code_tiles[i]
             wcols = slice(HALF * c, HALF * (c + 1))
-            bank = psum.tile([P, HALF], F32, name="acc%d" % s, tag="acc%d" % s, bufs=3)
-            for g in (0, 1):
-                cols = slice((2 * s + g) * P, (2 * s + g + 1) * P)
-                nc.tensor.matmul_mx(
-                    out=bank[:],
-                    lhsT=codes[:, cols].bitcast(E5X4),
-                    lhsT_scale=scales[:, cols],
-                    rhs=wcodes[s][:, g, wcols].bitcast(E5X4),
-                    rhs_scale=wscales[s][:, g, wcols],
-                    start=(g == 0),
-                    stop=(g == 1),
-                )
-            acc_tiles[(k, s)] = bank
-            if s == 0:
-                ss = stream.tile([P, 2 * HEADS], F32, name="ss", tag="ss", bufs=5)
-                junk = stream.tile([P, 2 * HEADS, DH], F32, name="junk", tag="junk", bufs=2)
-                sum_tiles[k] = (ss, junk)
-            ss, junk = sum_tiles[k]
-            for hh in range(HEADS):
-                nc.scalar.activation(
-                    out=junk[:, HEADS * s + hh, :],
-                    in_=bank[:, DH * hh : DH * (hh + 1)],
-                    func=ACT.Square,
-                    accum_out=ss[:, HEADS * s + hh : HEADS * s + hh + 1],
-                )
-
-        def norms(k):
-            ss = sum_tiles[k][0]
-            floor = stream.tile([P, 2 * HEADS], F32, name="floor", tag="floor", bufs=2)
+            acc = []
+            for s in (0, 1):
+                bank = psum.tile([P, HALF], F32, name="acc%d" % s, tag="acc%d" % s, bufs=3)
+                for g in (0, 1):
+                    cols = slice((2 * s + g) * P, (2 * s + g + 1) * P)
+                    nc.tensor.matmul_mx(
+                        out=bank[:],
+                        lhsT=codes[:, cols].bitcast(E5X4),
+                        lhsT_scale=scales[:, cols],
+                        rhs=wcodes[s][:, g, wcols].bitcast(E5X4),
+                        rhs_scale=wscales[s][:, g, wcols],
+                        start=(g == 0),
+                        stop=(g == 1),
+                    )
+                acc.append(bank)
+            ss = stream.tile([P, 2 * HEADS], F32, name="ss", tag="ss", bufs=4)
+            junk = stream.tile([P, 2 * HEADS, DH], F32, name="junk", tag="junk", bufs=2)
+            for s in (0, 1):
+                for hh in range(HEADS):
+                    nc.scalar.activation(
+                        out=junk[:, HEADS * s + hh, :],
+                        in_=acc[s][:, DH * hh : DH * (hh + 1)],
+                        func=ACT.Square,
+                        accum_out=ss[:, HEADS * s + hh : HEADS * s + hh + 1],
+                    )
+            floor = stream.tile([P, 2 * HEADS], F32, name="floor", tag="floor", bufs=4)
             nc.scalar.activation(out=floor[:], in_=ss[:], func=ACT.Relu, bias=neg_eps2[:, 0:1])
-            norm = stream.tile([P, 2 * HEADS], F32, name="norm", tag="norm", bufs=2)
-            nc.scalar.activation(out=norm[:], in_=floor[:], func=ACT.Sqrt, bias=pos_eps2[:, 0:1])
-            inv = stream.tile([P, 2 * HEADS], F32, name="inv", tag="inv", bufs=5)
-            nc.vector.reciprocal(out=inv[:], in_=norm[:])
-            inv_tiles[k] = inv
+            inv = stream.tile([P, 2 * HEADS], F32, name="inv", tag="inv", bufs=4)
+            nc.scalar.activation(out=inv[:], in_=floor[:], func=ACT.Abs_reciprocal_sqrt, bias=pos_eps2[:, 0:1])
+            unit_tiles[unit] = (acc, inv)
 
-        def rotate(k, s):
-            i, c = units[k]
+        def rotate(unit, next_tile, last):
+            i, c = unit
             t, b = divmod(i, B)
-            bank = acc_tiles[(k, s)]
-            inv = inv_tiles[k]
-            if s == 0:
-                xp = stream.tile([P, HEADS, 2 * DH], F32, name="xp", tag="xp", bufs=4)
-                yp = stream.tile([P, HEADS, 2 * DH], F32, name="yp", tag="yp", bufs=3)
-                prod_tiles[k] = (xp, yp)
-            xp, yp = prod_tiles[k]
+            acc, inv = unit_tiles[unit]
+            xp = stream.tile([P, HEADS, 2 * DH], F32, name="xp", tag="xp", bufs=4)
+            yp = stream.tile([P, HEADS, 2 * DH], F32, name="yp", tag="yp", bufs=3)
+            prod = (xp, yp)
+            dest = out[b, HEADS * c : HEADS * (c + 1), t * P : (t + 1) * P, :].rearrange("h n d -> n h d")
             for hh in range(HEADS):
-                nc.vector.scalar_tensor_tensor(
-                    out=prod_tiles[k][s][:, hh, :].rearrange("p (q j) -> p q j", q=2),
-                    in0=bank[:, DH * hh : DH * (hh + 1)].unsqueeze(1).to_broadcast([P, 2, DH]),
-                    scalar=inv[:, HEADS * s + hh : HEADS * s + hh + 1],
-                    in1=tables[t][s][:, HEADS * c + hh, :, :],
-                    op0=ALU.mult,
-                    op1=ALU.mult,
-                )
-                if s == 1 and hh % 4 == 3:
+                for s in (0, 1):
+                    if hh == 3 and s == 1 and next_tile is not None:
+                        quantise_tokens(next_tile)
+                    nc.vector.scalar_tensor_tensor(
+                        out=prod[s][:, hh, :].rearrange("p (q j) -> p q j", q=2),
+                        in0=acc[s][:, DH * hh : DH * (hh + 1)].unsqueeze(1).to_broadcast([P, 2, DH]),
+                        scalar=inv[:, HEADS * s + hh : HEADS * s + hh + 1],
+                        in1=tables[t][s][:, HEADS * c + hh, :, :],
+                        op0=ALU.mult,
+                        op1=ALU.mult,
+                    )
+                if hh % 4 == 3:
                     hs = slice(hh - 3, hh + 1)
                     nc.gpsimd.tensor_tensor(out=xp[:, hs, :], in0=xp[:, hs, :], in1=yp[:, hs, :], op=ALU.add)
-            if s == 1:
-                nc.sync.dma_start(
-                    out=out[b, HEADS * c : HEADS * (c + 1), t * P : (t + 1) * P, :].rearrange("h n d -> n h d"),
-                    in_=xp[:],
-                )
-
-        def later_angles(t):
-            cols = slice(t * P, (t + 1) * P)
-            cstep = step[:, 0, t - 1 : t]
-            sstep = step[:, 1, t - 1 : t]
-            cross = stream.tile([P, 2, P], F32, name="cross", tag="cross", bufs=2)
-            nc.vector.tensor_scalar(
-                out=cross[:, 0, :], in0=trig[:, 1, 0:P], scalar1=sstep, scalar2=None, op0=ALU.mult
-            )
-            nc.vector.tensor_scalar(
-                out=cross[:, 1, :], in0=trig[:, 0, 0:P], scalar1=sstep, scalar2=None, op0=ALU.mult
-            )
-            nc.vector.scalar_tensor_tensor(
-                out=trig[:, 0, cols], in0=trig[:, 0, 0:P], scalar=cstep, in1=cross[:, 0, :],
-                op0=ALU.mult, op1=ALU.subtract,
-            )
-            nc.vector.scalar_tensor_tensor(
-                out=trig[:, 1, cols], in0=trig[:, 1, 0:P], scalar=cstep, in1=cross[:, 1, :],
-                op0=ALU.mult, op1=ALU.add,
-            )
-            split_columns(t * P, (t + 1) * P)
-
-        def later_table(m):
-            table_piece(1 + m // 8, m % 8)
+                    if last:
+                        nc.sync.dma_start(out=dest[:, hs, :], in_=xp[:, hs, :])
+            if not last:
+                nc.sync.dma_start(out=dest, in_=xp[:])
 
         turn_tokens(0)
-        turn_tokens(1)
         quantise_tokens(0)
-        load_tokens(4)
         for s in (0, 1):
             for piece in (0, 1):
-                prep_weights(s, piece)
-        turn_tokens(2)
-        turn_tokens(3)
+                prep_weights(s, piece, False)
+        turn_tokens(1)
         quantise_tokens(1)
-        load_tokens(5)
         for e in range(8):
             table_piece(0, e)
-        for k in (0, 1):
-            project(k, 0)
-            project(k, 1)
-            norms(k)
-        for s in (0, 1):
-            for piece in (2, 3):
-                prep_weights(s, piece)
-        turn_tokens(4)
-        turn_tokens(5)
-        quantise_tokens(2)
-        later_angles(1)
-        later_table(0)
-        later_table(1)
-        project(2, 0)
-        project(2, 1)
-        norms(2)
 
-        n_units = len(units)
-        for k in range(n_units):
-            rotate(k, 0)
-            if k % 2 == 0 and k // 2 + 6 < TILES:
-                load_tokens(k // 2 + 6)
-            if k + 6 < 2 * TILES:
-                turn_tokens(k + 6)
-            if k % 2 == 0 and 3 <= k // 2 + 2 < TILES:
-                quantise_tokens(k // 2 + 2)
-            if k % 8 == 4 and k // 8 + 2 < T_TILES:
-                later_angles(k // 8 + 2)
-            if k + 2 < 8 * (T_TILES - 1):
-                later_table(k + 2)
-            if k + 3 < n_units:
-                project(k + 3, 0)
-            rotate(k, 1)
-            if k + 3 < n_units:
-                project(k + 3, 1)
-                norms(k + 3)
+        for t in range(1, T_TILES):
+            cols = slice(t * P, (t + 1) * P)
+            by_cos = stream.tile([P, 2, P], F32, name="by_cos", tag="by_cos", bufs=2)
+            by_sin = stream.tile([P, 2, P], F32, name="by_sin", tag="by_sin", bufs=2)
+            nc.gpsimd.tensor_scalar(
+                out=by_cos[:], in0=trig[:, :, 0:P], scalar1=step[:, 0, t - 1 : t], scalar2=0.0,
+                op0=ALU.mult, op1=ALU.add,
+            )
+            nc.gpsimd.tensor_scalar(
+                out=by_sin[:], in0=trig[:, :, 0:P], scalar1=step[:, 1, t - 1 : t], scalar2=0.0,
+                op0=ALU.mult, op1=ALU.add,
+            )
+            nc.gpsimd.tensor_tensor(out=trig[:, 0, cols], in0=by_cos[:, 0, :], in1=by_sin[:, 1, :], op=ALU.subtract)
+            nc.gpsimd.tensor_tensor(out=trig[:, 1, cols], in0=by_cos[:, 1, :], in1=by_sin[:, 0, :], op=ALU.add)
+            nc.gpsimd.tensor_scalar(
+                out=split[:, :, cols], in0=trig[:, :, cols], scalar1=1.0, scalar2=0.0, op0=ALU.mult, op1=ALU.add
+            )
+            nc.gpsimd.tensor_tensor(
+                out=split[DH:P, :, cols], in0=trig[DH:P, :, cols], in1=split[DH:P, :, cols], op=ALU.subtract
+            )
+
+        units = [(0, 0), (1, 0), (0, 1), (1, 1)] + [(i, c) for i in range(2, TILES) for c in (0, 1)]
+        project(units[0])
+        for k in range(len(units)):
+            if k + 1 < len(units):
+                project(units[k + 1])
+            due = k // 2 + 2 if (k % 2 == 1 and k // 2 + 2 < TILES) else None
+            rotate(units[k], due, k == len(units) - 1)
+            if k == 0:
+                for s in (0, 1):
+                    for piece in (2, 3):
+                        prep_weights(s, piece, True)
+            if k % 2 == 0:
+                if k // 2 + 4 < TILES:
+                    load_tokens(k // 2 + 4)
+                if k // 2 + 2 < TILES:
+                    turn_tokens(k // 2 + 2)
+            if k % 8 < 4 and k // 8 + 1 < T_TILES:
+                table_piece(k // 8 + 1, 2 * (k % 8))
+                table_piece(k // 8 + 1, 2 * (k % 8) + 1)

@@ -303,7 +303,7 @@ def tile_cmattention_pa_kernel(tc, x, a, Wq_x, Wq_a, qx_scale, qa_scale, out):
             dest = out[b, HEADS * c : HEADS * (c + 1), t * P : (t + 1) * P, :].rearrange("h n d -> n h d")
             for hh in range(HEADS):
                 for s in (0, 1):
-                    if hh == 3 and s == 1 and next_tile is not None:
+                    if hh == HEADS - 1 and s == 0 and next_tile is not None:
                         quantise_tokens(next_tile)
                     nc.vector.scalar_tensor_tensor(
                         out=prod[s][:, hh, :].rearrange("p (q j) -> p q j", q=2),
@@ -313,12 +313,13 @@ def tile_cmattention_pa_kernel(tc, x, a, Wq_x, Wq_a, qx_scale, qa_scale, out):
                         op0=ALU.mult,
                         op1=ALU.mult,
                     )
-                if hh % 4 == 3:
+                if last and hh % 4 == 3:
                     hs = slice(hh - 3, hh + 1)
-                    nc.gpsimd.tensor_tensor(out=xp[:, hs, :], in0=xp[:, hs, :], in1=yp[:, hs, :], op=ALU.add)
-                    if last:
-                        nc.sync.dma_start(out=dest[:, hs, :], in_=xp[:, hs, :])
+                    adder = nc.gpsimd if hh == 3 else nc.vector
+                    adder.tensor_tensor(out=xp[:, hs, :], in0=xp[:, hs, :], in1=yp[:, hs, :], op=ALU.add)
+                    nc.sync.dma_start(out=dest[:, hs, :], in_=xp[:, hs, :])
             if not last:
+                nc.gpsimd.tensor_tensor(out=xp[:], in0=xp[:], in1=yp[:], op=ALU.add)
                 nc.sync.dma_start(out=dest, in_=xp[:])
 
         turn_tokens(0)

@@ -303,8 +303,6 @@ def tile_cmattention_pa_kernel(tc, x, a, Wq_x, Wq_a, qx_scale, qa_scale, out):
             dest = out[b, HEADS * c : HEADS * (c + 1), t * P : (t + 1) * P, :].rearrange("h n d -> n h d")
             for hh in range(HEADS):
                 for s in (0, 1):
-                    if hh == HEADS - 1 and s == 0 and next_tile is not None:
-                        quantise_tokens(next_tile)
                     nc.vector.scalar_tensor_tensor(
                         out=prod[s][:, hh, :].rearrange("p (q j) -> p q j", q=2),
                         in0=acc[s][:, DH * hh : DH * (hh + 1)].unsqueeze(1).to_broadcast([P, 2, DH]),
@@ -318,6 +316,8 @@ def tile_cmattention_pa_kernel(tc, x, a, Wq_x, Wq_a, qx_scale, qa_scale, out):
                     adder = nc.gpsimd if hh == 3 else nc.vector
                     adder.tensor_tensor(out=xp[:, hs, :], in0=xp[:, hs, :], in1=yp[:, hs, :], op=ALU.add)
                     nc.sync.dma_start(out=dest[:, hs, :], in_=xp[:, hs, :])
+            if next_tile is not None:
+                quantise_tokens(next_tile)
             if not last:
                 nc.gpsimd.tensor_tensor(out=xp[:], in0=xp[:], in1=yp[:], op=ALU.add)
                 nc.sync.dma_start(out=dest, in_=xp[:])

@@ -117,20 +117,20 @@ def tile_cmattention_pa_kernel(tc, x, a, Wq_x, Wq_a, qx_scale, qa_scale, out):
             channel_multiplier=0,
             allow_small_or_imprecise_dtypes=True,
         )
-        y = const.tile([P, 2, NB], F32, name="y", tag="y")
+        y = stream.tile([P, 2, NB], F32, name="y", tag="xp", bufs=4)
         nc.vector.tensor_scalar(out=y[:, 0, :], in0=nb[:], scalar1=turns[:, 0:1], scalar2=None, op0=ALU.mult)
         nc.vector.tensor_scalar(
             out=y[:, 1, :], in0=nb[:], scalar1=turns[:, 0:1], scalar2=0.75, op0=ALU.mult, op1=ALU.add
         )
-        ki = const.tile([P, 2, NB], I32, name="ki", tag="ki")
+        ki = stream.tile([P, 2, NB], I32, name="ki", tag="xp", bufs=4)
         nc.vector.tensor_copy(out=ki[:], in_=y[:])
-        kf = const.tile([P, 2, NB], F32, name="kf", tag="kf")
+        kf = stream.tile([P, 2, NB], F32, name="kf", tag="xp", bufs=4)
         nc.vector.tensor_copy(out=kf[:], in_=ki[:])
-        frac = const.tile([P, 2, NB], F32, name="frac", tag="frac")
+        frac = stream.tile([P, 2, NB], F32, name="frac", tag="xp", bufs=4)
         nc.vector.tensor_tensor(out=frac[:], in0=y[:], in1=kf[:], op=ALU.subtract)
-        half_sin = const.tile([P, 2, NB], F32, name="half_sin", tag="half_sin")
+        half_sin = stream.tile([P, 2, NB], F32, name="half_sin", tag="yp", bufs=3)
         nc.scalar.activation(out=half_sin[:], in_=frac[:], func=ACT.Sin, scale=PI)
-        sq = const.tile([P, 2, NB], F32, name="sq", tag="sq")
+        sq = stream.tile([P, 2, NB], F32, name="sq", tag="yp", bufs=3)
         nc.scalar.activation(out=sq[:], in_=half_sin[:], func=ACT.Square)
         nc.scalar.activation(out=warm[:], in_=sq[:, 0, 0:1], func=ACT.Abs_reciprocal_sqrt, bias=one[:, 0:1])
 
@@ -233,29 +233,32 @@ def tile_cmattention_pa_kernel(tc, x, a, Wq_x, Wq_a, qx_scale, qa_scale, out):
             nc.vector.quantize_mx(out=codes[:].bitcast(E5X4), scales=scales[:], in_=grouped[:])
             code_tiles[i] = (codes, scales)
 
-        def prep_weights(s, piece, on_vector):
-            wr = wraw_tiles[(s, piece)]
-            words = wr[:].rearrange("p c k -> p (c k)").bitcast(F32)
-            cols = slice(256 * piece, 256 * (piece + 1))
+        def prep_weights(s, c, on_vector):
             for g in (0, 1):
-                bank = psum.tile([P, 2, 2, P], F32, name="wbank", tag="tp", bufs=2)
-                for c in (0, 1):
-                    for u in (0, 1):
-                        lo = 512 * c + 256 * g
-                        nc.tensor.transpose(bank[:, c, u, :], words[:, lo + u : lo + 256 : 2], ident_f[:])
-                wg = stream.tile([P, D], BF16, name="wg", tag="wg", bufs=3, align_bytes=64)
-                if on_vector and g == 1:
-                    nc.vector.tensor_copy(
-                        out=wg[:].bitcast(F32).rearrange("p (c r u) -> p c r u", c=2, u=2),
-                        in_=bank[:].rearrange("p c u r -> p c r u"),
-                    )
-                else:
-                    nc.scalar.copy(
-                        out=wg[:].bitcast(F32).rearrange("p (c r u) -> p c r u", c=2, u=2),
-                        in_=bank[:].rearrange("p c u r -> p c r u"),
-                    )
+                wg = stream.tile([P, 2, D], BF16, name="wg", tag="wg", bufs=2, align_bytes=64)
+                for half in (0, 1):
+                    wr = wraw_tiles[(s, 2 * c + half)]
+                    words = wr[:].rearrange("p c k -> p (c k)").bitcast(F32)
+                    bank = psum.tile([P, 2, 2, P], F32, name="wbank", tag="tp", bufs=2)
+                    for r in (0, 1):
+                        for u in (0, 1):
+                            lo = 512 * r + 256 * g
+                            nc.tensor.transpose(bank[:, r, u, :], words[:, lo + u : lo + 256 : 2], ident_f[:])
+                    if on_vector and g == 1:
+                        nc.vector.tensor_copy(
+                            out=wg[:, half, :].bitcast(F32).rearrange("p (c r u) -> p c r u", c=2, u=2),
+                            in_=bank[:].rearrange("p c u r -> p c r u"),
+                        )
+                    else:
+                        nc.scalar.copy(
+                            out=wg[:, half, :].bitcast(F32).rearrange("p (c r u) -> p c r u", c=2, u=2),
+                            in_=bank[:].rearrange("p c u r -> p c r u"),
+                        )
+                cols = slice(HALF * c, HALF * (c + 1))
                 nc.vector.quantize_mx(
-                    out=wcodes[s][:, g, cols].bitcast(E5X4), scales=wscales[s][:, g, cols], in_=wg[:]
+                    out=wcodes[s][:, g, cols].bitcast(E5X4),
+                    scales=wscales[s][:, g, cols],
+                    in_=wg[:].rearrange("p h k -> p (h k)"),
                 )
 
         def project(unit):
@@ -325,33 +328,44 @@ def tile_cmattention_pa_kernel(tc, x, a, Wq_x, Wq_a, qx_scale, qa_scale, out):
         turn_tokens(0)
         quantise_tokens(0)
         for s in (0, 1):
-            for piece in (0, 1):
-                prep_weights(s, piece, False)
+            prep_weights(s, 0, True)
         turn_tokens(1)
         quantise_tokens(1)
         for e in range(8):
             table_piece(0, e)
 
-        for t in range(1, T_TILES):
+        angle_tiles = {}
+
+        def later_angles(t, step_no):
             cols = slice(t * P, (t + 1) * P)
-            by_cos = stream.tile([P, 2, P], F32, name="by_cos", tag="by_cos", bufs=2)
-            by_sin = stream.tile([P, 2, P], F32, name="by_sin", tag="by_sin", bufs=2)
-            nc.gpsimd.tensor_scalar(
-                out=by_cos[:], in0=trig[:, :, 0:P], scalar1=step[:, 0, t - 1 : t], scalar2=0.0,
-                op0=ALU.mult, op1=ALU.add,
-            )
-            nc.gpsimd.tensor_scalar(
-                out=by_sin[:], in0=trig[:, :, 0:P], scalar1=step[:, 1, t - 1 : t], scalar2=0.0,
-                op0=ALU.mult, op1=ALU.add,
-            )
-            nc.gpsimd.tensor_tensor(out=trig[:, 0, cols], in0=by_cos[:, 0, :], in1=by_sin[:, 1, :], op=ALU.subtract)
-            nc.gpsimd.tensor_tensor(out=trig[:, 1, cols], in0=by_cos[:, 1, :], in1=by_sin[:, 0, :], op=ALU.add)
-            nc.gpsimd.tensor_scalar(
-                out=split[:, :, cols], in0=trig[:, :, cols], scalar1=1.0, scalar2=0.0, op0=ALU.mult, op1=ALU.add
-            )
-            nc.gpsimd.tensor_tensor(
-                out=split[DH:P, :, cols], in0=trig[DH:P, :, cols], in1=split[DH:P, :, cols], op=ALU.subtract
-            )
+            if step_no == 0:
+                by_cos = stream.tile([P, 2, P], F32, name="by_cos", tag="by_cos", bufs=2)
+                by_sin = stream.tile([P, 2, P], F32, name="by_sin", tag="by_sin", bufs=2)
+                angle_tiles[t] = (by_cos, by_sin)
+                nc.gpsimd.tensor_scalar(
+                    out=by_cos[:], in0=trig[:, :, 0:P], scalar1=step[:, 0, t - 1 : t], scalar2=0.0,
+                    op0=ALU.mult, op1=ALU.add,
+                )
+                nc.gpsimd.tensor_scalar(
+                    out=by_sin[:], in0=trig[:, :, 0:P], scalar1=step[:, 1, t - 1 : t], scalar2=0.0,
+                    op0=ALU.mult, op1=ALU.add,
+                )
+            by_cos, by_sin = angle_tiles[t]
+            if step_no == 1:
+                nc.gpsimd.tensor_tensor(
+                    out=trig[:, 0, cols], in0=by_cos[:, 0, :], in1=by_sin[:, 1, :], op=ALU.subtract
+                )
+                nc.gpsimd.tensor_tensor(out=trig[:, 1, cols], in0=by_cos[:, 1, :], in1=by_sin[:, 0, :], op=ALU.add)
+            if step_no == 2:
+                nc.gpsimd.tensor_scalar(
+                    out=split[:, :, cols], in0=trig[:, :, cols], scalar1=1.0, scalar2=0.0, op0=ALU.mult, op1=ALU.add
+                )
+                nc.gpsimd.tensor_tensor(
+                    out=split[DH:P, :, cols], in0=trig[DH:P, :, cols], in1=split[DH:P, :, cols], op=ALU.subtract
+                )
+
+        for step_no in range(3):
+            later_angles(1, step_no)
 
         units = [(0, 0), (1, 0), (0, 1), (1, 1)] + [(i, c) for i in range(2, TILES) for c in (0, 1)]
         project(units[0])
@@ -362,8 +376,9 @@ def tile_cmattention_pa_kernel(tc, x, a, Wq_x, Wq_a, qx_scale, qa_scale, out):
             rotate(units[k], due, k == len(units) - 1)
             if k == 0:
                 for s in (0, 1):
-                    for piece in (2, 3):
-                        prep_weights(s, piece, True)
+                    prep_weights(s, 1, True)
+            if k % 2 == 0 and k // 6 + 2 < T_TILES:
+                later_angles(k // 6 + 2, (k % 6) // 2)
             if k % 2 == 0:
                 if k // 2 + 4 < TILES:
                     load_tokens(k // 2 + 4)

@@ -69,10 +69,17 @@ def tile_cmattention_pa_kernel(tc, x, a, Wq_x, Wq_a, qx_scale, qa_scale, out):
         load_tokens(2)
         load_tokens(3)
 
+        gpad = const.tile([P, P], BF16, name="gpad", tag="gpad")
+        nc.vector.memset(gpad[:], 0.0)
+        for s in (0, 1):
+            rows = gains[s].rearrange("h o d -> h (o d)")
+            for i in (0, 1):
+                nc.scalar.dma_start(out=gpad[H * s : H * (s + 1), DH * i : DH * (i + 1)], in_=rows)
         ident_f = const.tile([P, P], F32, name="ident_f", tag="ident_f")
-        make_identity(nc, ident_f[:])
+        nc.vector.memset(ident_f[:], 0.0)
+        make_identity(nc, ident_f[:], nomemset=True)
         ident_b = const.tile([P, P], BF16, name="ident_b", tag="ident_b")
-        make_identity(nc, ident_b[:])
+        nc.vector.tensor_copy(out=ident_b[:], in_=ident_f[:])
 
         one = const.tile([P, 1], F32, name="one", tag="one")
         nc.vector.memset(one[:], 1.0)
@@ -152,12 +159,6 @@ def tile_cmattention_pa_kernel(tc, x, a, Wq_x, Wq_a, qx_scale, qa_scale, out):
 
         split_columns(0, P)
 
-        gpad = const.tile([P, P], BF16, name="gpad", tag="gpad")
-        nc.gpsimd.memset(gpad[:], 0.0)
-        for s in (0, 1):
-            rows = gains[s].rearrange("h o d -> h (o d)")
-            for i in (0, 1):
-                nc.scalar.dma_start(out=gpad[H * s : H * (s + 1), DH * i : DH * (i + 1)], in_=rows)
         gps = psum.tile([P, P], BF16, name="gps", tag="tp", bufs=2)
         nc.tensor.transpose(gps[:], gpad[:], ident_b[:])
         gcol = const.tile([P, 2 * H], BF16, name="gcol", tag="gcol")

@@ -36,6 +36,14 @@ def tile_cmattention_pa_kernel(tc, x, a, Wq_x, Wq_a, qx_scale, qa_scale, out):
         stream = ctx.enter_context(tc.tile_pool(name="stream", bufs=1))
         psum = ctx.enter_context(tc.psum_pool(name="psum", bufs=1))
 
+        state = {"work": (0, 1, 2, 3, 4, 5, 6, 7), "n": 0}
+
+        def work_bank(shape, dtype, name):
+            banks = state["work"]
+            b = banks[state["n"] % len(banks)]
+            state["n"] = state["n"] + 1
+            return psum.tile(shape, dtype, name=name, tag="b%d" % b, bufs=1)
+
         raw_tiles = {}
         wraw_tiles = {}
         code_tiles = {}
@@ -56,6 +64,12 @@ def tile_cmattention_pa_kernel(tc, x, a, Wq_x, Wq_a, qx_scale, qa_scale, out):
             )
             wraw_tiles[(s, piece)] = wr
 
+        gpad = const.tile([P, P], BF16, name="gpad", tag="gpad")
+        nc.vector.memset(gpad[:], 0.0)
+        for s in (0, 1):
+            rows = gains[s].rearrange("h o d -> h (o d)")
+            for i in (0, 1):
+                nc.sync.dma_start(out=gpad[H * s : H * (s + 1), DH * i : DH * (i + 1)], in_=rows)
         load_tokens(0)
         load_weights(0, 0)
         load_weights(0, 1)
@@ -69,12 +83,6 @@ def tile_cmattention_pa_kernel(tc, x, a, Wq_x, Wq_a, qx_scale, qa_scale, out):
         load_tokens(2)
         load_tokens(3)
 
-        gpad = const.tile([P, P], BF16, name="gpad", tag="gpad")
-        nc.vector.memset(gpad[:], 0.0)
-        for s in (0, 1):
-            rows = gains[s].rearrange("h o d -> h (o d)")
-            for i in (0, 1):
-                nc.scalar.dma_start(out=gpad[H * s : H * (s + 1), DH * i : DH * (i + 1)], in_=rows)
         ident_f = const.tile([P, P], F32, name="ident_f", tag="ident_f")
         nc.vector.memset(ident_f[:], 0.0)
         make_identity(nc, ident_f[:], nomemset=True)
@@ -98,19 +106,15 @@ def tile_cmattention_pa_kernel(tc, x, a, Wq_x, Wq_a, qx_scale, qa_scale, out):
             wcodes.append(wc)
             wscales.append(ws)
 
-        frow = const.tile([P, P], F32, name="frow", tag="frow")
-        nc.vector.memset(frow[:, 0:1], 1.0)
-        for m in (1, 2, 4, 8, 16, 32):
-            nc.vector.tensor_scalar(
-                out=frow[:, m : 2 * m], in0=frow[:, 0:m], scalar1=RATIO**m, scalar2=None, op0=ALU.mult
-            )
-        nc.vector.tensor_copy(out=frow[:, DH : 2 * DH], in_=frow[:, 0:DH])
-        fps = psum.tile([P, P], F32, name="fps", tag="tp", bufs=2)
-        nc.tensor.transpose(fps[:], frow[:], ident_f[:])
-        turns = const.tile([P, 1], F32, name="turns", tag="turns")
-        nc.vector.tensor_scalar(
-            out=turns[:], in0=fps[:, 0:1], scalar1=1.0 / (2.0 * PI), scalar2=None, op0=ALU.mult
-        )
+        frow = const.tile([P, 2, DH], F32, name="frow", tag="frow")
+        nc.vector.memset(frow[:, :, 0:1], 1.0)
+        for width in (1, 4, 16):
+            for m in (width, 2 * width, 3 * width):
+                nc.vector.tensor_scalar(
+                    out=frow[:, :, m : m + width], in0=frow[:, :, 0:width], scalar1=RATIO**m, scalar2=None, op0=ALU.mult
+                )
+        fps = work_bank([P, P], F32, "fps")
+        nc.tensor.transpose(fps[:], frow[:].rearrange("p a j -> p (a j)"), ident_f[:])
 
         NB = P + T_TILES - 1
         nb = const.tile([P, NB], F32, name="nb", tag="nb")
@@ -124,17 +128,19 @@ def tile_cmattention_pa_kernel(tc, x, a, Wq_x, Wq_a, qx_scale, qa_scale, out):
             channel_multiplier=0,
             allow_small_or_imprecise_dtypes=True,
         )
+        nbt = const.tile([P, NB], F32, name="nbt", tag="nbt")
+        nc.gpsimd.tensor_scalar(
+            out=nbt[:], in0=nb[:], scalar1=1.0 / (2.0 * PI), scalar2=0.0, op0=ALU.mult, op1=ALU.add
+        )
         y = stream.tile([P, 2, NB], F32, name="y", tag="xp", bufs=4)
-        nc.vector.tensor_scalar(out=y[:, 0, :], in0=nb[:], scalar1=turns[:, 0:1], scalar2=None, op0=ALU.mult)
+        nc.vector.tensor_scalar(out=y[:, 0, :], in0=nbt[:], scalar1=fps[:, 0:1], scalar2=None, op0=ALU.mult)
         nc.vector.tensor_scalar(
-            out=y[:, 1, :], in0=nb[:], scalar1=turns[:, 0:1], scalar2=0.75, op0=ALU.mult, op1=ALU.add
+            out=y[:, 1, :], in0=nbt[:], scalar1=fps[:, 0:1], scalar2=0.75, op0=ALU.mult, op1=ALU.add
         )
         ki = stream.tile([P, 2, NB], I32, name="ki", tag="xp", bufs=4)
         nc.vector.tensor_copy(out=ki[:], in_=y[:])
-        kf = stream.tile([P, 2, NB], F32, name="kf", tag="xp", bufs=4)
-        nc.vector.tensor_copy(out=kf[:], in_=ki[:])
         frac = stream.tile([P, 2, NB], F32, name="frac", tag="xp", bufs=4)
-        nc.vector.tensor_tensor(out=frac[:], in0=y[:], in1=kf[:], op=ALU.subtract)
+        nc.vector.tensor_tensor(out=frac[:], in0=y[:], in1=ki[:], op=ALU.subtract)
         half_sin = stream.tile([P, 2, NB], F32, name="half_sin", tag="yp", bufs=3)
         nc.scalar.activation(out=half_sin[:], in_=frac[:], func=ACT.Sin, scale=PI)
         sq = stream.tile([P, 2, NB], F32, name="sq", tag="yp", bufs=3)
@@ -159,7 +165,7 @@ def tile_cmattention_pa_kernel(tc, x, a, Wq_x, Wq_a, qx_scale, qa_scale, out):
 
         split_columns(0, P)
 
-        gps = psum.tile([P, P], BF16, name="gps", tag="tp", bufs=2)
+        gps = work_bank([P, P], BF16, "gps")
         nc.tensor.transpose(gps[:], gpad[:], ident_b[:])
         gcol = const.tile([P, 2 * H], BF16, name="gcol", tag="gcol")
         nc.vector.tensor_copy(out=gcol[:], in_=gps[:, 0 : 2 * H])
@@ -187,7 +193,7 @@ def tile_cmattention_pa_kernel(tc, x, a, Wq_x, Wq_a, qx_scale, qa_scale, out):
         def table_piece(t, e):
             kind, s, q, sign = parts[e // 2]
             h0 = HEADS * (e % 2)
-            ps = psum.tile([P, HALF], F32, name="tps", tag="tp", bufs=2)
+            ps = work_bank([P, HALF], F32, "tps")
             nc.tensor.matmul(
                 out=ps[:],
                 lhsT=split[:, kind, t * P : (t + 1) * P],
@@ -219,7 +225,7 @@ def tile_cmattention_pa_kernel(tc, x, a, Wq_x, Wq_a, qx_scale, qa_scale, out):
             grouped = stream.tile([P, 2 * D], BF16, name="grouped", tag="grouped", bufs=3, align_bytes=64)
             gwords = grouped[:].bitcast(F32).rearrange("p (s g r u) -> p s g r u", s=2, g=2, u=2)
             for s in (0, 1):
-                bank = psum.tile([P, 2, 2, P], F32, name="bank", tag="tp", bufs=2)
+                bank = work_bank([P, 2, 2, P], F32, "bank")
                 for g in (0, 1):
                     for u in (0, 1):
                         lo = 512 * s + 256 * g
@@ -240,7 +246,7 @@ def tile_cmattention_pa_kernel(tc, x, a, Wq_x, Wq_a, qx_scale, qa_scale, out):
                 for half in (0, 1):
                     wr = wraw_tiles[(s, 2 * c + half)]
                     words = wr[:].rearrange("p c k -> p (c k)").bitcast(F32)
-                    bank = psum.tile([P, 2, 2, P], F32, name="wbank", tag="tp", bufs=2)
+                    bank = work_bank([P, 2, 2, P], F32, "wbank")
                     for r in (0, 1):
                         for u in (0, 1):
                             lo = 512 * r + 256 * g
@@ -262,13 +268,13 @@ def tile_cmattention_pa_kernel(tc, x, a, Wq_x, Wq_a, qx_scale, qa_scale, out):
                     in_=wg[:].rearrange("p h k -> p (h k)"),
                 )
 
-        def project(unit):
+        def project(unit, pair):
             i, c = unit
             codes, scales = code_tiles[i]
             wcols = slice(HALF * c, HALF * (c + 1))
             acc = []
             for s in (0, 1):
-                bank = psum.tile([P, HALF], F32, name="acc%d" % s, tag="acc%d" % s, bufs=3)
+                bank = psum.tile([P, HALF], F32, name="acc%d" % s, tag="b%d" % (2 * pair + s), bufs=1)
                 for g in (0, 1):
                     cols = slice((2 * s + g) * P, (2 * s + g + 1) * P)
                     nc.tensor.matmul_mx(
@@ -369,15 +375,26 @@ def tile_cmattention_pa_kernel(tc, x, a, Wq_x, Wq_a, qx_scale, qa_scale, out):
             later_angles(1, step_no)
 
         units = [(0, 0), (1, 0), (0, 1), (1, 1)] + [(i, c) for i in range(2, TILES) for c in (0, 1)]
-        project(units[0])
+        EARLY = 0
+
+        def pair_of(u):
+            return u % 2 if u < EARLY else u % 3
+
+        state["work"] = (6, 7)
+        state["n"] = 0
+        project(units[0], pair_of(0))
+        state["work"] = (4, 5, 6, 7)
+        for s in (0, 1):
+            prep_weights(s, 1, True)
+        state["work"] = (6, 7)
         for k in range(len(units)):
+            if k == 4:
+                state["work"] = (6, 7)
+                state["n"] = 0
             if k + 1 < len(units):
-                project(units[k + 1])
+                project(units[k + 1], pair_of(k + 1))
             due = k // 2 + 2 if (k % 2 == 1 and k // 2 + 2 < TILES) else None
             rotate(units[k], due, k == len(units) - 1)
-            if k == 0:
-                for s in (0, 1):
-                    prep_weights(s, 1, True)
             if k % 2 == 0 and k // 6 + 2 < T_TILES:
                 later_angles(k // 6 + 2, (k % 6) // 2)
             if k % 2 == 0:

@@ -57,7 +57,7 @@ def tile_cmattention_pa_kernel(tc, x, a, Wq_x, Wq_a, qx_scale, qa_scale, out):
             raw_tiles[i] = raw
 
         def load_weights(s, piece):
-            wr = stream.tile([P, 2, D], BF16, name="wr", tag="wr", bufs=8)
+            wr = stream.tile([P, 2, D], BF16, name="wr", tag="wr", bufs=6)
             nc.sync.dma_start(
                 out=wr[:],
                 in_=weights[s][piece * 256 : (piece + 1) * 256, :].rearrange("(c p) k -> p c k", p=P),
@@ -132,14 +132,14 @@ def tile_cmattention_pa_kernel(tc, x, a, Wq_x, Wq_a, qx_scale, qa_scale, out):
         nc.gpsimd.tensor_scalar(
             out=nbt[:], in0=nb[:], scalar1=1.0 / (2.0 * PI), scalar2=0.0, op0=ALU.mult, op1=ALU.add
         )
-        y = stream.tile([P, 2, NB], F32, name="y", tag="xp", bufs=4)
+        y = stream.tile([P, 2, NB], F32, name="y", tag="xp", bufs=5)
         nc.vector.tensor_scalar(out=y[:, 0, :], in0=nbt[:], scalar1=fps[:, 0:1], scalar2=None, op0=ALU.mult)
         nc.vector.tensor_scalar(
             out=y[:, 1, :], in0=nbt[:], scalar1=fps[:, 0:1], scalar2=0.75, op0=ALU.mult, op1=ALU.add
         )
-        ki = stream.tile([P, 2, NB], I32, name="ki", tag="xp", bufs=4)
+        ki = stream.tile([P, 2, NB], I32, name="ki", tag="xp", bufs=5)
         nc.vector.tensor_copy(out=ki[:], in_=y[:])
-        frac = stream.tile([P, 2, NB], F32, name="frac", tag="xp", bufs=4)
+        frac = stream.tile([P, 2, NB], F32, name="frac", tag="xp", bufs=5)
         nc.vector.tensor_tensor(out=frac[:], in0=y[:], in1=ki[:], op=ALU.subtract)
         half_sin = stream.tile([P, 2, NB], F32, name="half_sin", tag="yp", bufs=3)
         nc.scalar.activation(out=half_sin[:], in_=frac[:], func=ACT.Sin, scale=PI)
@@ -241,11 +241,15 @@ def tile_cmattention_pa_kernel(tc, x, a, Wq_x, Wq_a, qx_scale, qa_scale, out):
             code_tiles[i] = (codes, scales)
 
         def prep_weights(s, c, on_vector):
+            wgs = []
             for g in (0, 1):
-                wg = stream.tile([P, 2, D], BF16, name="wg", tag="wg", bufs=2, align_bytes=64)
-                for half in (0, 1):
-                    wr = wraw_tiles[(s, 2 * c + half)]
-                    words = wr[:].rearrange("p c k -> p (c k)").bitcast(F32)
+                wg = stream.tile([P, 2, D], BF16, name="wg", tag="wg", bufs=4, align_bytes=64)
+                wgs.append(wg)
+            for half in (0, 1):
+                wr = wraw_tiles[(s, 2 * c + half)]
+                words = wr[:].rearrange("p c k -> p (c k)").bitcast(F32)
+                for g in (0, 1):
+                    wg = wgs[g]
                     bank = work_bank([P, 2, 2, P], F32, "wbank")
                     for r in (0, 1):
                         for u in (0, 1):
@@ -261,11 +265,12 @@ def tile_cmattention_pa_kernel(tc, x, a, Wq_x, Wq_a, qx_scale, qa_scale, out):
                             out=wg[:, half, :].bitcast(F32).rearrange("p (c r u) -> p c r u", c=2, u=2),
                             in_=bank[:].rearrange("p c u r -> p c r u"),
                         )
-                cols = slice(HALF * c, HALF * (c + 1))
+            cols = slice(HALF * c, HALF * (c + 1))
+            for g in (0, 1):
                 nc.vector.quantize_mx(
                     out=wcodes[s][:, g, cols].bitcast(E5X4),
                     scales=wscales[s][:, g, cols],
-                    in_=wg[:].rearrange("p h k -> p (h k)"),
+                    in_=wgs[g][:].rearrange("p h k -> p (h k)"),
                 )
 
         def project(unit, pair):
@@ -307,7 +312,7 @@ def tile_cmattention_pa_kernel(tc, x, a, Wq_x, Wq_a, qx_scale, qa_scale, out):
             i, c = unit
             t, b = divmod(i, B)
             acc, inv = unit_tiles[unit]
-            xp = stream.tile([P, HEADS, 2 * DH], F32, name="xp", tag="xp", bufs=4)
+            xp = stream.tile([P, HEADS, 2 * DH], F32, name="xp", tag="xp", bufs=5)
             yp = stream.tile([P, HEADS, 2 * DH], F32, name="yp", tag="yp", bufs=3)
             prod = (xp, yp)
             dest = out[b, HEADS * c : HEADS * (c + 1), t * P : (t + 1) * P, :].rearrange("h n d -> n h d")

@@ -407,6 +407,5 @@ def tile_cmattention_pa_kernel(tc, x, a, Wq_x, Wq_a, qx_scale, qa_scale, out):
                     load_tokens(k // 2 + 4)
                 if k // 2 + 2 < TILES:
                     turn_tokens(k // 2 + 2)
-            if k % 8 < 4 and k // 8 + 1 < T_TILES:
-                table_piece(k // 8 + 1, 2 * (k % 8))
-                table_piece(k // 8 + 1, 2 * (k % 8) + 1)
+            if k // 8 + 1 < T_TILES:
+                table_piece(k // 8 + 1, k % 8)

@@ -219,19 +219,21 @@ def tile_cmattention_pa_kernel(tc, x, a, Wq_x, Wq_a, qx_scale, qa_scale, out):
 
         group_tiles = {}
 
-        def turn_tokens(i):
+        def turn_tokens(i, streams=(0, 1)):
             raw = raw_tiles[i]
             words = raw[:].rearrange("p s k -> p (s k)").bitcast(F32)
-            grouped = stream.tile([P, 2 * D], BF16, name="grouped", tag="grouped", bufs=3, align_bytes=64)
+            if 0 in streams:
+                grouped = stream.tile([P, 2 * D], BF16, name="grouped", tag="grouped", bufs=3, align_bytes=64)
+                group_tiles[i] = grouped
+            grouped = group_tiles[i]
             gwords = grouped[:].bitcast(F32).rearrange("p (s g r u) -> p s g r u", s=2, g=2, u=2)
-            for s in (0, 1):
+            for s in streams:
                 bank = work_bank([P, 2, 2, P], F32, "bank")
                 for g in (0, 1):
                     for u in (0, 1):
                         lo = 512 * s + 256 * g
                         nc.tensor.transpose(bank[:, g, u, :], words[:, lo + u : lo + 256 : 2], ident_f[:])
                 nc.scalar.copy(out=gwords[:, s], in_=bank[:].rearrange("p g u r -> p g r u"))
-            group_tiles[i] = grouped
 
         def quantise_tokens(i):
             grouped = group_tiles[i]
@@ -399,6 +401,8 @@ def tile_cmattention_pa_kernel(tc, x, a, Wq_x, Wq_a, qx_scale, qa_scale, out):
             if k + 1 < len(units):
                 project(units[k + 1], pair_of(k + 1))
             due = k // 2 + 2 if (k % 2 == 1 and k // 2 + 2 < TILES) else None
+            if due is not None:
+                turn_tokens(due, (1,))
             rotate(units[k], due, k == len(units) - 1)
             if k % 2 == 0 and k // 6 + 2 < T_TILES:
                 later_angles(k // 6 + 2, (k % 6) // 2)
@@ -406,6 +410,6 @@ def tile_cmattention_pa_kernel(tc, x, a, Wq_x, Wq_a, qx_scale, qa_scale, out):
                 if k // 2 + 4 < TILES:
                     load_tokens(k // 2 + 4)
                 if k // 2 + 2 < TILES:
-                    turn_tokens(k // 2 + 2)
+                    turn_tokens(k // 2 + 2, (0,))
             if k // 8 + 1 < T_TILES:
                 table_piece(k // 8 + 1, k % 8)

@@ -356,30 +356,35 @@ def tile_cmattention_pa_kernel(tc, x, a, Wq_x, Wq_a, qx_scale, qa_scale, out):
                 by_cos = stream.tile([P, 2, P], F32, name="by_cos", tag="by_cos", bufs=2)
                 by_sin = stream.tile([P, 2, P], F32, name="by_sin", tag="by_sin", bufs=2)
                 angle_tiles[t] = (by_cos, by_sin)
+            by_cos, by_sin = angle_tiles[t]
+            if step_no == 0:
                 nc.gpsimd.tensor_scalar(
                     out=by_cos[:], in0=trig[:, :, 0:P], scalar1=step[:, 0, t - 1 : t], scalar2=0.0,
                     op0=ALU.mult, op1=ALU.add,
                 )
+            if step_no == 1:
                 nc.gpsimd.tensor_scalar(
                     out=by_sin[:], in0=trig[:, :, 0:P], scalar1=step[:, 1, t - 1 : t], scalar2=0.0,
                     op0=ALU.mult, op1=ALU.add,
                 )
-            by_cos, by_sin = angle_tiles[t]
-            if step_no == 1:
+            if step_no == 2:
                 nc.gpsimd.tensor_tensor(
                     out=trig[:, 0, cols], in0=by_cos[:, 0, :], in1=by_sin[:, 1, :], op=ALU.subtract
                 )
+            if step_no == 3:
                 nc.gpsimd.tensor_tensor(out=trig[:, 1, cols], in0=by_cos[:, 1, :], in1=by_sin[:, 0, :], op=ALU.add)
-            if step_no == 2:
+            if step_no == 4:
                 nc.gpsimd.tensor_scalar(
                     out=split[:, :, cols], in0=trig[:, :, cols], scalar1=1.0, scalar2=0.0, op0=ALU.mult, op1=ALU.add
                 )
+            if step_no == 5:
                 nc.gpsimd.tensor_tensor(
                     out=split[DH:P, :, cols], in0=trig[DH:P, :, cols], in1=split[DH:P, :, cols], op=ALU.subtract
                 )
 
-        for step_no in range(3):
-            later_angles(1, step_no)
+        for t in (1, 2):
+            for step_no in range(6):
+                later_angles(t, step_no)
 
         units = [(0, 0), (1, 0), (0, 1), (1, 1)] + [(i, c) for i in range(2, TILES) for c in (0, 1)]
         EARLY = 0
@@ -404,8 +409,8 @@ def tile_cmattention_pa_kernel(tc, x, a, Wq_x, Wq_a, qx_scale, qa_scale, out):
             if due is not None:
                 turn_tokens(due, (1,))
             rotate(units[k], due, k == len(units) - 1)
-            if k % 2 == 0 and k // 6 + 2 < T_TILES:
-                later_angles(k // 6 + 2, (k % 6) // 2)
+            if k % 2 == 1 and k // 12 + 3 < T_TILES:
+                later_angles(k // 12 + 3, (k % 12) // 2)
             if k % 2 == 0:
                 if k // 2 + 4 < TILES:
                     load_tokens(k // 2 + 4)

@@ -190,10 +190,13 @@ def tile_cmattention_pa_kernel(tc, x, a, Wq_x, Wq_a, qx_scale, qa_scale, out):
 
         parts = ((0, 0, 0, 1.0), (1, 0, 1, 1.0), (1, 1, 0, -1.0), (0, 1, 1, 1.0))
 
-        def table_piece(t, e):
+        table_banks = {}
+
+        def table_matmul(t, e):
             kind, s, q, sign = parts[e // 2]
             h0 = HEADS * (e % 2)
             ps = work_bank([P, HALF], F32, "tps")
+            table_banks[(t, e)] = ps
             nc.tensor.matmul(
                 out=ps[:],
                 lhsT=split[:, kind, t * P : (t + 1) * P],
@@ -201,7 +204,12 @@ def tile_cmattention_pa_kernel(tc, x, a, Wq_x, Wq_a, qx_scale, qa_scale, out):
                 start=True,
                 stop=True,
             )
-            if e % 2 == 0:
+
+        def table_copy(t, e, on_vector):
+            kind, s, q, sign = parts[e // 2]
+            h0 = HEADS * (e % 2)
+            ps = table_banks[(t, e)]
+            if on_vector:
                 nc.vector.tensor_scalar(
                     out=tables[t][s][:, h0 : h0 + HEADS, q, :],
                     in0=ps[:].rearrange("p (h j) -> p h j", j=DH),
@@ -234,6 +242,24 @@ def tile_cmattention_pa_kernel(tc, x, a, Wq_x, Wq_a, qx_scale, qa_scale, out):
                         lo = 512 * s + 256 * g
                         nc.tensor.transpose(bank[:, g, u, :], words[:, lo + u : lo + 256 : 2], ident_f[:])
                 nc.scalar.copy(out=gwords[:, s], in_=bank[:].rearrange("p g u r -> p g r u"))
+
+        bank_tiles = {}
+
+        def turn_start(i, s):
+            words = raw_tiles[i][:].rearrange("p s k -> p (s k)").bitcast(F32)
+            bank = work_bank([P, 2, 2, P], F32, "bank")
+            bank_tiles[(i, s)] = bank
+            for g in (0, 1):
+                for u in (0, 1):
+                    lo = 512 * s + 256 * g
+                    nc.tensor.transpose(bank[:, g, u, :], words[:, lo + u : lo + 256 : 2], ident_f[:])
+
+        def turn_finish(i, s):
+            if i not in group_tiles:
+                grouped = stream.tile([P, 2 * D], BF16, name="grouped", tag="grouped", bufs=3, align_bytes=64)
+                group_tiles[i] = grouped
+            gwords = group_tiles[i][:].bitcast(F32).rearrange("p (s g r u) -> p s g r u", s=2, g=2, u=2)
+            nc.scalar.copy(out=gwords[:, s], in_=bank_tiles[(i, s)][:].rearrange("p g u r -> p g r u"))
 
         def quantise_tokens(i):
             grouped = group_tiles[i]
@@ -346,7 +372,8 @@ def tile_cmattention_pa_kernel(tc, x, a, Wq_x, Wq_a, qx_scale, qa_scale, out):
         turn_tokens(1)
         quantise_tokens(1)
         for e in range(8):
-            table_piece(0, e)
+            table_matmul(0, e)
+            table_copy(0, e, e % 2 == 0)
 
         angle_tiles = {}
 
@@ -399,22 +426,37 @@ def tile_cmattention_pa_kernel(tc, x, a, Wq_x, Wq_a, qx_scale, qa_scale, out):
         for s in (0, 1):
             prep_weights(s, 1, True)
         state["work"] = (6, 7)
-        for k in range(len(units)):
-            if k == 4:
-                state["work"] = (6, 7)
-                state["n"] = 0
+        state["n"] = 0
+
+        def tokens_behind(j):
+            return ((j + 5) // 2, 0) if j % 2 == 1 else ((j + 4) // 2, 1)
+
+        def side_start(j):
+            i, s = tokens_behind(j)
+            if i < TILES:
+                turn_start(i, s)
+            if j >= 0 and j // 8 + 1 < T_TILES:
+                table_matmul(j // 8 + 1, j % 8)
+
+        def side_finish(j):
+            i, s = tokens_behind(j)
+            if i < TILES:
+                turn_finish(i, s)
+            if j >= 0 and j // 8 + 1 < T_TILES:
+                table_copy(j // 8 + 1, j % 8, j % 2 == 1)
+
+        def step_of(k):
+            side_finish(k - 1)
             if k + 1 < len(units):
                 project(units[k + 1], pair_of(k + 1))
             due = k // 2 + 2 if (k % 2 == 1 and k // 2 + 2 < TILES) else None
-            if due is not None:
-                turn_tokens(due, (1,))
             rotate(units[k], due, k == len(units) - 1)
             if k % 2 == 1 and k // 12 + 3 < T_TILES:
                 later_angles(k // 12 + 3, (k % 12) // 2)
-            if k % 2 == 0:
-                if k // 2 + 4 < TILES:
-                    load_tokens(k // 2 + 4)
-                if k // 2 + 2 < TILES:
-                    turn_tokens(k // 2 + 2, (0,))
-            if k // 8 + 1 < T_TILES:
-                table_piece(k // 8 + 1, k % 8)
+            if k % 2 == 0 and k // 2 + 4 < TILES:
+                load_tokens(k // 2 + 4)
+            side_start(k)
+
+        side_start(-1)
+        for k in range(len(units)):
+            step_of(k)

@@ -254,12 +254,15 @@ def tile_cmattention_pa_kernel(tc, x, a, Wq_x, Wq_a, qx_scale, qa_scale, out):
                     lo = 512 * s + 256 * g
                     nc.tensor.transpose(bank[:, g, u, :], words[:, lo + u : lo + 256 : 2], ident_f[:])
 
-        def turn_finish(i, s):
+        def turn_finish(i, s, lo_token, hi_token):
             if i not in group_tiles:
                 grouped = stream.tile([P, 2 * D], BF16, name="grouped", tag="grouped", bufs=3, align_bytes=64)
                 group_tiles[i] = grouped
             gwords = group_tiles[i][:].bitcast(F32).rearrange("p (s g r u) -> p s g r u", s=2, g=2, u=2)
-            nc.scalar.copy(out=gwords[:, s], in_=bank_tiles[(i, s)][:].rearrange("p g u r -> p g r u"))
+            nc.scalar.copy(
+                out=gwords[:, s, :, lo_token:hi_token, :],
+                in_=bank_tiles[(i, s)][:, :, :, lo_token:hi_token].rearrange("p g u r -> p g r u"),
+            )
 
         def quantise_tokens(i):
             grouped = group_tiles[i]
@@ -301,7 +304,10 @@ def tile_cmattention_pa_kernel(tc, x, a, Wq_x, Wq_a, qx_scale, qa_scale, out):
                     in_=wgs[g][:].rearrange("p h k -> p (h k)"),
                 )
 
-        def project(unit, pair):
+        acc_tiles = {}
+        norm_tiles = {}
+
+        def matmuls(unit, pair):
             i, c = unit
             codes, scales = code_tiles[i]
             wcols = slice(HALF * c, HALF * (c + 1))
@@ -320,7 +326,12 @@ def tile_cmattention_pa_kernel(tc, x, a, Wq_x, Wq_a, qx_scale, qa_scale, out):
                         stop=(g == 1),
                     )
                 acc.append(bank)
+            acc_tiles[unit] = acc
+
+        def squares(unit):
+            acc = acc_tiles[unit]
             ss = stream.tile([P, 2 * HEADS], F32, name="ss", tag="ss", bufs=4)
+            norm_tiles[unit] = ss
             junk = stream.tile([P, 2 * HEADS, DH], F32, name="junk", tag="junk", bufs=2)
             for s in (0, 1):
                 for hh in range(HEADS):
@@ -330,11 +341,24 @@ def tile_cmattention_pa_kernel(tc, x, a, Wq_x, Wq_a, qx_scale, qa_scale, out):
                         func=ACT.Square,
                         accum_out=ss[:, HEADS * s + hh : HEADS * s + hh + 1],
                     )
+
+        def clamp(unit):
             floor = stream.tile([P, 2 * HEADS], F32, name="floor", tag="floor", bufs=4)
-            nc.scalar.activation(out=floor[:], in_=ss[:], func=ACT.Relu, bias=neg_eps2[:, 0:1])
+            nc.scalar.activation(out=floor[:], in_=norm_tiles[unit][:], func=ACT.Relu, bias=neg_eps2[:, 0:1])
+            norm_tiles[unit] = floor
+
+        def invert(unit):
             inv = stream.tile([P, 2 * HEADS], F32, name="inv", tag="inv", bufs=4)
-            nc.scalar.activation(out=inv[:], in_=floor[:], func=ACT.Abs_reciprocal_sqrt, bias=pos_eps2[:, 0:1])
-            unit_tiles[unit] = (acc, inv)
+            nc.scalar.activation(
+                out=inv[:], in_=norm_tiles[unit][:], func=ACT.Abs_reciprocal_sqrt, bias=pos_eps2[:, 0:1]
+            )
+            unit_tiles[unit] = (acc_tiles[unit], inv)
+
+        def project(unit, pair):
+            matmuls(unit, pair)
+            squares(unit)
+            clamp(unit)
+            invert(unit)
 
         def rotate(unit, next_tile, last):
             i, c = unit
@@ -354,16 +378,15 @@ def tile_cmattention_pa_kernel(tc, x, a, Wq_x, Wq_a, qx_scale, qa_scale, out):
                         op0=ALU.mult,
                         op1=ALU.mult,
                     )
-                if last and hh % 4 == 3:
-                    hs = slice(hh - 3, hh + 1)
-                    adder = nc.gpsimd if hh == 3 else nc.vector
-                    adder.tensor_tensor(out=xp[:, hs, :], in0=xp[:, hs, :], in1=yp[:, hs, :], op=ALU.add)
-                    nc.sync.dma_start(out=dest[:, hs, :], in_=xp[:, hs, :])
             if next_tile is not None:
                 quantise_tokens(next_tile)
             if not last:
                 nc.gpsimd.tensor_tensor(out=xp[:], in0=xp[:], in1=yp[:], op=ALU.add)
                 nc.sync.dma_start(out=dest, in_=xp[:])
+            if last:
+                for hs in (slice(0, 6), slice(6, 8)):
+                    nc.vector.tensor_tensor(out=xp[:, hs, :], in0=xp[:, hs, :], in1=yp[:, hs, :], op=ALU.add)
+                    nc.sync.dma_start(out=dest[:, hs, :], in_=xp[:, hs, :])
 
         turn_tokens(0)
         quantise_tokens(0)
@@ -422,6 +445,7 @@ def tile_cmattention_pa_kernel(tc, x, a, Wq_x, Wq_a, qx_scale, qa_scale, out):
         state["work"] = (6, 7)
         state["n"] = 0
         project(units[0], pair_of(0))
+        matmuls(units[1], pair_of(1))
         state["work"] = (4, 5, 6, 7)
         for s in (0, 1):
             prep_weights(s, 1, True)
@@ -429,7 +453,7 @@ def tile_cmattention_pa_kernel(tc, x, a, Wq_x, Wq_a, qx_scale, qa_scale, out):
         state["n"] = 0
 
         def tokens_behind(j):
-            return ((j + 5) // 2, 0) if j % 2 == 1 else ((j + 4) // 2, 1)
+            return ((j + 6) // 2, 0) if j % 2 == 0 else ((j + 5) // 2, 1)
 
         def side_start(j):
             i, s = tokens_behind(j)
@@ -438,25 +462,40 @@ def tile_cmattention_pa_kernel(tc, x, a, Wq_x, Wq_a, qx_scale, qa_scale, out):
             if j >= 0 and j // 8 + 1 < T_TILES:
                 table_matmul(j // 8 + 1, j % 8)
 
-        def side_finish(j):
-            i, s = tokens_behind(j)
-            if i < TILES:
-                turn_finish(i, s)
-            if j >= 0 and j // 8 + 1 < T_TILES:
-                table_copy(j // 8 + 1, j % 8, j % 2 == 1)
-
         def step_of(k):
-            side_finish(k - 1)
-            if k + 1 < len(units):
-                project(units[k + 1], pair_of(k + 1))
+            if k + 2 < len(units):
+                matmuls(units[k + 2], pair_of(k + 2))
+            j = k - 1
+            i, s = tokens_behind(j)
+            has_tokens = i < TILES
+            has_table = j >= 0 and j // 8 + 1 < T_TILES
+            scalar_table = has_table and j % 2 == 0
+            has_next = k + 1 < len(units)
+            if has_next:
+                squares(units[k + 1])
+            if has_tokens:
+                turn_finish(i, s, 0, P if scalar_table else P // 2)
+            if has_next:
+                clamp(units[k + 1])
+            if scalar_table:
+                table_copy(j // 8 + 1, j % 8, False)
+            elif has_tokens:
+                turn_finish(i, s, P // 2, P)
+            if has_next:
+                invert(units[k + 1])
             due = k // 2 + 2 if (k % 2 == 1 and k // 2 + 2 < TILES) else None
             rotate(units[k], due, k == len(units) - 1)
+            if has_table and not scalar_table:
+                table_copy(j // 8 + 1, j % 8, True)
             if k % 2 == 1 and k // 12 + 3 < T_TILES:
                 later_angles(k // 12 + 3, (k % 12) // 2)
             if k % 2 == 0 and k // 2 + 4 < TILES:
                 load_tokens(k // 2 + 4)
             side_start(k)
 
+        turn_tokens(2, (0,))
         side_start(-1)
-        for k in range(len(units)):
-            step_of(k)
+        pinned = {mybir.EngineType.PE, mybir.EngineType.Activation, mybir.EngineType.DVE, mybir.EngineType.Pool}
+        with tc.manual_schedule(engines=pinned):
+            for k in range(len(units)):
+                step_of(k)

@@ -469,7 +469,7 @@ def tile_cmattention_pa_kernel(tc, x, a, Wq_x, Wq_a, qx_scale, qa_scale, out):
             i, s = tokens_behind(j)
             has_tokens = i < TILES
             has_table = j >= 0 and j // 8 + 1 < T_TILES
-            scalar_table = has_table and j % 2 == 0
+            scalar_table = has_table and (j % 2 == 0 or j % 4 == 3)
             has_next = k + 1 < len(units)
             if has_next:
                 squares(units[k + 1])

@@ -432,7 +432,7 @@ def tile_cmattention_pa_kernel(tc, x, a, Wq_x, Wq_a, qx_scale, qa_scale, out):
                     out=split[DH:P, :, cols], in0=trig[DH:P, :, cols], in1=split[DH:P, :, cols], op=ALU.subtract
                 )
 
-        for t in (1, 2):
+        for t in range(1, T_TILES):
             for step_no in range(6):
                 later_angles(t, step_no)
 
@@ -487,8 +487,6 @@ def tile_cmattention_pa_kernel(tc, x, a, Wq_x, Wq_a, qx_scale, qa_scale, out):
             rotate(units[k], due, k == len(units) - 1)
             if has_table and not scalar_table:
                 table_copy(j // 8 + 1, j % 8, True)
-            if k % 2 == 1 and k // 12 + 3 < T_TILES:
-                later_angles(k // 12 + 3, (k % 12) // 2)
             if k % 2 == 0 and k // 2 + 4 < TILES:
                 load_tokens(k // 2 + 4)
             side_start(k)

@@ -396,7 +396,7 @@ def tile_cmattention_pa_kernel(tc, x, a, Wq_x, Wq_a, qx_scale, qa_scale, out):
         quantise_tokens(1)
         for e in range(8):
             table_matmul(0, e)
-            table_copy(0, e, e % 2 == 0)
+            table_copy(0, e, e % 4 == 0)
 
         angle_tiles = {}
 
@@ -448,7 +448,7 @@ def tile_cmattention_pa_kernel(tc, x, a, Wq_x, Wq_a, qx_scale, qa_scale, out):
         matmuls(units[1], pair_of(1))
         state["work"] = (4, 5, 6, 7)
         for s in (0, 1):
-            prep_weights(s, 1, True)
+            prep_weights(s, 1, False)
         state["work"] = (6, 7)
         state["n"] = 0
 

@@ -264,12 +264,18 @@ def tile_cmattention_pa_kernel(tc, x, a, Wq_x, Wq_a, qx_scale, qa_scale, out):
                 in_=bank_tiles[(i, s)][:, :, :, lo_token:hi_token].rearrange("p g u r -> p g r u"),
             )
 
-        def quantise_tokens(i):
+        def quantise_tokens(i, streams=(0, 1)):
             grouped = group_tiles[i]
-            codes = stream.tile([P, 4 * P], U32, name="codes", tag="codes", bufs=4, align_bytes=64)
-            scales = stream.tile([P, 4 * P], U8, name="scales", tag="scales", bufs=4, align_bytes=64)
-            nc.vector.quantize_mx(out=codes[:].bitcast(E5X4), scales=scales[:], in_=grouped[:])
-            code_tiles[i] = (codes, scales)
+            if i not in code_tiles:
+                codes = stream.tile([P, 4 * P], U32, name="codes", tag="codes", bufs=4, align_bytes=64)
+                scales = stream.tile([P, 4 * P], U8, name="scales", tag="scales", bufs=4, align_bytes=64)
+                code_tiles[i] = (codes, scales)
+            codes, scales = code_tiles[i]
+            lo = 2 * P * streams[0]
+            hi = 2 * P * (streams[-1] + 1)
+            nc.vector.quantize_mx(
+                out=codes[:, lo:hi].bitcast(E5X4), scales=scales[:, lo:hi], in_=grouped[:, 4 * lo : 4 * hi]
+            )
 
         def prep_weights(s, c, on_vector):
             wgs = []
@@ -307,26 +313,27 @@ def tile_cmattention_pa_kernel(tc, x, a, Wq_x, Wq_a, qx_scale, qa_scale, out):
         acc_tiles = {}
         norm_tiles = {}
 
-        def matmuls(unit, pair):
+        def matmul_stream(unit, pair, s):
             i, c = unit
             codes, scales = code_tiles[i]
             wcols = slice(HALF * c, HALF * (c + 1))
-            acc = []
+            bank = psum.tile([P, HALF], F32, name="acc%d" % s, tag="b%d" % (2 * pair + s), bufs=1)
+            for g in (0, 1):
+                cols = slice((2 * s + g) * P, (2 * s + g + 1) * P)
+                nc.tensor.matmul_mx(
+                    out=bank[:],
+                    lhsT=codes[:, cols].bitcast(E5X4),
+                    lhsT_scale=scales[:, cols],
+                    rhs=wcodes[s][:, g, wcols].bitcast(E5X4),
+                    rhs_scale=wscales[s][:, g, wcols],
+                    start=(g == 0),
+                    stop=(g == 1),
+                )
+            acc_tiles.setdefault(unit, {})[s] = bank
+
+        def matmuls(unit, pair):
             for s in (0, 1):
-                bank = psum.tile([P, HALF], F32, name="acc%d" % s, tag="b%d" % (2 * pair + s), bufs=1)
-                for g in (0, 1):
-                    cols = slice((2 * s + g) * P, (2 * s + g + 1) * P)
-                    nc.tensor.matmul_mx(
-                        out=bank[:],
-                        lhsT=codes[:, cols].bitcast(E5X4),
-                        lhsT_scale=scales[:, cols],
-                        rhs=wcodes[s][:, g, wcols].bitcast(E5X4),
-                        rhs_scale=wscales[s][:, g, wcols],
-                        start=(g == 0),
-                        stop=(g == 1),
-                    )
-                acc.append(bank)
-            acc_tiles[unit] = acc
+                matmul_stream(unit, pair, s)
 
         def squares(unit):
             acc = acc_tiles[unit]
@@ -360,7 +367,7 @@ def tile_cmattention_pa_kernel(tc, x, a, Wq_x, Wq_a, qx_scale, qa_scale, out):
             clamp(unit)
             invert(unit)
 
-        def rotate(unit, next_tile, last):
+        def rotate(unit, next_tile, last, between=None):
             i, c = unit
             t, b = divmod(i, B)
             acc, inv = unit_tiles[unit]
@@ -368,18 +375,20 @@ def tile_cmattention_pa_kernel(tc, x, a, Wq_x, Wq_a, qx_scale, qa_scale, out):
             yp = stream.tile([P, HEADS, 2 * DH], F32, name="yp", tag="yp", bufs=3)
             prod = (xp, yp)
             dest = out[b, HEADS * c : HEADS * (c + 1), t * P : (t + 1) * P, :].rearrange("h n d -> n h d")
-            for hh in range(HEADS):
-                for s in (0, 1):
-                    nc.vector.scalar_tensor_tensor(
-                        out=prod[s][:, hh, :].rearrange("p (q j) -> p q j", q=2),
-                        in0=acc[s][:, DH * hh : DH * (hh + 1)].unsqueeze(1).to_broadcast([P, 2, DH]),
-                        scalar=inv[:, HEADS * s + hh : HEADS * s + hh + 1],
-                        in1=tables[t][s][:, HEADS * c + hh, :, :],
-                        op0=ALU.mult,
-                        op1=ALU.mult,
-                    )
+            order = [(hh, s) for hh in range(HEADS) for s in (0, 1)] if last else [(hh, s) for s in (0, 1) for hh in range(HEADS)]
+            for n_done, (hh, s) in enumerate(order):
+                if n_done == HEADS and between is not None:
+                    between()
+                nc.vector.scalar_tensor_tensor(
+                    out=prod[s][:, hh, :].rearrange("p (q j) -> p q j", q=2),
+                    in0=acc[s][:, DH * hh : DH * (hh + 1)].unsqueeze(1).to_broadcast([P, 2, DH]),
+                    scalar=inv[:, HEADS * s + hh : HEADS * s + hh + 1],
+                    in1=tables[t][s][:, HEADS * c + hh, :, :],
+                    op0=ALU.mult,
+                    op1=ALU.mult,
+                )
             if next_tile is not None:
-                quantise_tokens(next_tile)
+                quantise_tokens(next_tile[0], (next_tile[1],))
             if not last:
                 nc.gpsimd.tensor_tensor(out=xp[:], in0=xp[:], in1=yp[:], op=ALU.add)
                 nc.sync.dma_start(out=dest, in_=xp[:])
@@ -464,7 +473,7 @@ def tile_cmattention_pa_kernel(tc, x, a, Wq_x, Wq_a, qx_scale, qa_scale, out):
 
         def step_of(k):
             if k + 2 < len(units):
-                matmuls(units[k + 2], pair_of(k + 2))
+                matmul_stream(units[k + 2], pair_of(k + 2), 1)
             j = k - 1
             i, s = tokens_behind(j)
             has_tokens = i < TILES
@@ -483,14 +492,18 @@ def tile_cmattention_pa_kernel(tc, x, a, Wq_x, Wq_a, qx_scale, qa_scale, out):
                 turn_finish(i, s, P // 2, P)
             if has_next:
                 invert(units[k + 1])
-            due = k // 2 + 2 if (k % 2 == 1 and k // 2 + 2 < TILES) else None
-            rotate(units[k], due, k == len(units) - 1)
+            due = ((k + 4) // 2, 0) if k % 2 == 0 else ((k + 3) // 2, 1)
+            if due[0] >= TILES:
+                due = None
+            early = (lambda: matmul_stream(units[k + 3], pair_of(k + 3), 0)) if k + 3 < len(units) else None
+            rotate(units[k], due, k == len(units) - 1, early)
             if has_table and not scalar_table:
                 table_copy(j // 8 + 1, j % 8, True)
             if k % 2 == 0 and k // 2 + 4 < TILES:
                 load_tokens(k // 2 + 4)
             side_start(k)
 
+        matmul_stream(units[2], pair_of(2), 0)
         turn_tokens(2, (0,))
         side_start(-1)
         pinned = {mybir.EngineType.PE, mybir.EngineType.Activation, mybir.EngineType.DVE, mybir.EngineType.Pool}

@@ -375,10 +375,14 @@ def tile_cmattention_pa_kernel(tc, x, a, Wq_x, Wq_a, qx_scale, qa_scale, out):
             yp = stream.tile([P, HEADS, 2 * DH], F32, name="yp", tag="yp", bufs=3)
             prod = (xp, yp)
             dest = out[b, HEADS * c : HEADS * (c + 1), t * P : (t + 1) * P, :].rearrange("h n d -> n h d")
-            order = [(hh, s) for hh in range(HEADS) for s in (0, 1)] if last else [(hh, s) for s in (0, 1) for hh in range(HEADS)]
+            by_head = last or between is None
+            order = [(hh, s) for hh in range(HEADS) for s in (0, 1)] if by_head else [(hh, s) for s in (0, 1) for hh in range(HEADS)]
             for n_done, (hh, s) in enumerate(order):
                 if n_done == HEADS and between is not None:
                     between()
+                if n_done == HEADS and by_head and not last:
+                    nc.gpsimd.tensor_tensor(out=xp[:, 0:4, :], in0=xp[:, 0:4, :], in1=yp[:, 0:4, :], op=ALU.add)
+                    nc.sync.dma_start(out=dest[:, 0:4, :], in_=xp[:, 0:4, :])
                 nc.vector.scalar_tensor_tensor(
                     out=prod[s][:, hh, :].rearrange("p (q j) -> p q j", q=2),
                     in0=acc[s][:, DH * hh : DH * (hh + 1)].unsqueeze(1).to_broadcast([P, 2, DH]),
@@ -389,7 +393,10 @@ def tile_cmattention_pa_kernel(tc, x, a, Wq_x, Wq_a, qx_scale, qa_scale, out):
                 )
             if next_tile is not None:
                 quantise_tokens(next_tile[0], (next_tile[1],))
-            if not last:
+            if by_head and not last:
+                nc.gpsimd.tensor_tensor(out=xp[:, 4:8, :], in0=xp[:, 4:8, :], in1=yp[:, 4:8, :], op=ALU.add)
+                nc.sync.dma_start(out=dest[:, 4:8, :], in_=xp[:, 4:8, :])
+            elif not last:
                 nc.gpsimd.tensor_tensor(out=xp[:], in0=xp[:], in1=yp[:], op=ALU.add)
                 nc.sync.dma_start(out=dest, in_=xp[:])
             if last:

@@ -64,13 +64,13 @@ def tile_cmattention_pa_kernel(tc, x, a, Wq_x, Wq_a, qx_scale, qa_scale, out):
             )
             wraw_tiles[(s, piece)] = wr
 
+        load_tokens(0)
         gpad = const.tile([P, P], BF16, name="gpad", tag="gpad")
         nc.vector.memset(gpad[:], 0.0)
         for s in (0, 1):
             rows = gains[s].rearrange("h o d -> h (o d)")
             for i in (0, 1):
                 nc.sync.dma_start(out=gpad[H * s : H * (s + 1), DH * i : DH * (i + 1)], in_=rows)
-        load_tokens(0)
         load_weights(0, 0)
         load_weights(0, 1)
         load_weights(1, 0)
@@ -217,6 +217,8 @@ def tile_cmattention_pa_kernel(tc, x, a, Wq_x, Wq_a, qx_scale, qa_scale, out):
                     scalar2=None,
                     op0=ALU.mult,
                 )
+            elif sign == 1.0:
+                nc.scalar.copy(out=tables[t][s][:, h0 : h0 + HEADS, q, :], in_=ps[:].rearrange("p (h j) -> p h j", j=DH))
             else:
                 nc.scalar.activation(
                     out=tables[t][s][:, h0 : h0 + HEADS, q, :],
@@ -367,7 +369,7 @@ def tile_cmattention_pa_kernel(tc, x, a, Wq_x, Wq_a, qx_scale, qa_scale, out):
             clamp(unit)
             invert(unit)
 
-        def rotate(unit, next_tile, last, between=None):
+        def rotate(unit, next_tile, last, between=None, split_add=False):
             i, c = unit
             t, b = divmod(i, B)
             acc, inv = unit_tiles[unit]
@@ -375,7 +377,7 @@ def tile_cmattention_pa_kernel(tc, x, a, Wq_x, Wq_a, qx_scale, qa_scale, out):
             yp = stream.tile([P, HEADS, 2 * DH], F32, name="yp", tag="yp", bufs=3)
             prod = (xp, yp)
             dest = out[b, HEADS * c : HEADS * (c + 1), t * P : (t + 1) * P, :].rearrange("h n d -> n h d")
-            by_head = last or between is None
+            by_head = last or split_add
             order = [(hh, s) for hh in range(HEADS) for s in (0, 1)] if by_head else [(hh, s) for s in (0, 1) for hh in range(HEADS)]
             for n_done, (hh, s) in enumerate(order):
                 if n_done == HEADS and between is not None:
@@ -503,7 +505,7 @@ def tile_cmattention_pa_kernel(tc, x, a, Wq_x, Wq_a, qx_scale, qa_scale, out):
             if due[0] >= TILES:
                 due = None
             early = (lambda: matmul_stream(units[k + 3], pair_of(k + 3), 0)) if k + 3 < len(units) else None
-            rotate(units[k], due, k == len(units) - 1, early)
+            rotate(units[k], due, k == len(units) - 1, early, k == len(units) - 2)
             if has_table and not scalar_table:
                 table_copy(j // 8 + 1, j % 8, True)
             if k % 2 == 0 and k // 2 + 4 < TILES:

@@ -341,7 +341,7 @@ def tile_cmattention_pa_kernel(tc, x, a, Wq_x, Wq_a, qx_scale, qa_scale, out):
             acc = acc_tiles[unit]
             ss = stream.tile([P, 2 * HEADS], F32, name="ss", tag="ss", bufs=4)
             norm_tiles[unit] = ss
-            junk = stream.tile([P, 2 * HEADS, DH], F32, name="junk", tag="junk", bufs=2)
+            junk = stream.tile([P, 2 * HEADS, DH], BF16, name="junk", tag="junk", bufs=2)
             for s in (0, 1):
                 for hh in range(HEADS):
                     nc.scalar.activation(

@@ -450,9 +450,36 @@ def tile_cmattention_pa_kernel(tc, x, a, Wq_x, Wq_a, qx_scale, qa_scale, out):
                     out=split[DH:P, :, cols], in0=trig[DH:P, :, cols], in1=split[DH:P, :, cols], op=ALU.subtract
                 )
 
-        for t in range(1, T_TILES):
-            for step_no in range(6):
-                later_angles(t, step_no)
+        for step_no in range(6):
+            later_angles(1, step_no)
+
+        REST = T_TILES - 2
+        rest = slice(2 * P, T_TILES * P)
+        all_cos = stream.tile([P, REST, 2, P], F32, name="all_cos", tag="xp", bufs=5)
+        all_sin = stream.tile([P, REST, 2, P], F32, name="all_sin", tag="xp", bufs=5)
+        for t in range(2, T_TILES):
+            nc.gpsimd.tensor_scalar(
+                out=all_cos[:, t - 2], in0=trig[:, :, 0:P], scalar1=step[:, 0, t - 1 : t], scalar2=0.0,
+                op0=ALU.mult, op1=ALU.add,
+            )
+            nc.gpsimd.tensor_scalar(
+                out=all_sin[:, t - 2], in0=trig[:, :, 0:P], scalar1=step[:, 1, t - 1 : t], scalar2=0.0,
+                op0=ALU.mult, op1=ALU.add,
+            )
+        nc.gpsimd.tensor_tensor(
+            out=trig[:, 0, rest].rearrange("p (t r) -> p t r", r=P), in0=all_cos[:, :, 0, :], in1=all_sin[:, :, 1, :],
+            op=ALU.subtract,
+        )
+        nc.gpsimd.tensor_tensor(
+            out=trig[:, 1, rest].rearrange("p (t r) -> p t r", r=P), in0=all_cos[:, :, 1, :], in1=all_sin[:, :, 0, :],
+            op=ALU.add,
+        )
+        nc.gpsimd.tensor_scalar(
+            out=split[:, :, rest], in0=trig[:, :, rest], scalar1=1.0, scalar2=0.0, op0=ALU.mult, op1=ALU.add
+        )
+        nc.gpsimd.tensor_tensor(
+            out=split[DH:P, :, rest], in0=trig[DH:P, :, rest], in1=split[DH:P, :, rest], op=ALU.subtract
+        )
 
         units = [(0, 0), (1, 0), (0, 1), (1, 1)] + [(i, c) for i in range(2, TILES) for c in (0, 1)]
         EARLY = 0

@@ -453,11 +453,11 @@ def tile_cmattention_pa_kernel(tc, x, a, Wq_x, Wq_a, qx_scale, qa_scale, out):
         for step_no in range(6):
             later_angles(1, step_no)
 
-        REST = T_TILES - 2
-        rest = slice(2 * P, T_TILES * P)
+        REST = 2
+        rest = slice(2 * P, (2 + REST) * P)
         all_cos = stream.tile([P, REST, 2, P], F32, name="all_cos", tag="xp", bufs=5)
         all_sin = stream.tile([P, REST, 2, P], F32, name="all_sin", tag="xp", bufs=5)
-        for t in range(2, T_TILES):
+        for t in range(2, 2 + REST):
             nc.gpsimd.tensor_scalar(
                 out=all_cos[:, t - 2], in0=trig[:, :, 0:P], scalar1=step[:, 0, t - 1 : t], scalar2=0.0,
                 op0=ALU.mult, op1=ALU.add,
@@ -535,6 +535,8 @@ def tile_cmattention_pa_kernel(tc, x, a, Wq_x, Wq_a, qx_scale, qa_scale, out):
             rotate(units[k], due, k == len(units) - 1, early, k == len(units) - 2)
             if has_table and not scalar_table:
                 table_copy(j // 8 + 1, j % 8, True)
+                if k // 4 < 6:
+                    later_angles(T_TILES - 1, k // 4)
             if k % 2 == 0 and k // 2 + 4 < TILES:
                 load_tokens(k // 2 + 4)
             side_start(k)

@@ -493,7 +493,7 @@ def tile_cmattention_pa_kernel(tc, x, a, Wq_x, Wq_a, qx_scale, qa_scale, out):
         matmuls(units[1], pair_of(1))
         state["work"] = (4, 5, 6, 7)
         for s in (0, 1):
-            prep_weights(s, 1, False)
+            prep_weights(s, 1, s == 1)
         state["work"] = (6, 7)
         state["n"] = 0
 

@@ -450,20 +450,18 @@ def tile_cmattention_pa_kernel(tc, x, a, Wq_x, Wq_a, qx_scale, qa_scale, out):
                     out=split[DH:P, :, cols], in0=trig[DH:P, :, cols], in1=split[DH:P, :, cols], op=ALU.subtract
                 )
 
-        for step_no in range(6):
-            later_angles(1, step_no)
-
-        REST = 2
-        rest = slice(2 * P, (2 + REST) * P)
+        FIRST = 1
+        REST = 3
+        rest = slice(FIRST * P, (FIRST + REST) * P)
         all_cos = stream.tile([P, REST, 2, P], F32, name="all_cos", tag="xp", bufs=5)
         all_sin = stream.tile([P, REST, 2, P], F32, name="all_sin", tag="xp", bufs=5)
-        for t in range(2, 2 + REST):
+        for t in range(FIRST, FIRST + REST):
             nc.gpsimd.tensor_scalar(
-                out=all_cos[:, t - 2], in0=trig[:, :, 0:P], scalar1=step[:, 0, t - 1 : t], scalar2=0.0,
+                out=all_cos[:, t - FIRST], in0=trig[:, :, 0:P], scalar1=step[:, 0, t - 1 : t], scalar2=0.0,
                 op0=ALU.mult, op1=ALU.add,
             )
             nc.gpsimd.tensor_scalar(
-                out=all_sin[:, t - 2], in0=trig[:, :, 0:P], scalar1=step[:, 1, t - 1 : t], scalar2=0.0,
+                out=all_sin[:, t - FIRST], in0=trig[:, :, 0:P], scalar1=step[:, 1, t - 1 : t], scalar2=0.0,
                 op0=ALU.mult, op1=ALU.add,
             )
         nc.gpsimd.tensor_tensor(

from contextlib import ExitStack

import concourse.mybir as mybir
from concourse.masks import make_identity

B, N, D, H, DH = 4, 640, 1024, 16, 64
P = 128
FLOPS = 2 * 2 * B * N * D * H * DH

F32 = mybir.dt.float32
BF16 = mybir.dt.bfloat16
I32 = mybir.dt.int32
U32 = mybir.dt.uint32
U8 = mybir.dt.uint8
E5X4 = mybir.dt.float8_e5m2_x4
ACT = mybir.ActivationFunctionType
ALU = mybir.AluOpType

PI = 3.141592653589793
RATIO = 10000.0 ** (-1.0 / DH)
EPS2 = 1e-24
T_TILES = N // P
TILES = B * T_TILES
HALF = 512
HEADS = HALF // DH


def tile_cmattention_pa_kernel(tc, x, a, Wq_x, Wq_a, qx_scale, qa_scale, out):
    nc = tc.nc
    acts = (x, a)
    weights = (Wq_x, Wq_a)
    gains = (qx_scale, qa_scale)

    with ExitStack() as ctx:
        const = ctx.enter_context(tc.tile_pool(name="const", bufs=1))
        stream = ctx.enter_context(tc.tile_pool(name="stream", bufs=1))
        psum = ctx.enter_context(tc.psum_pool(name="psum", bufs=1))

        state = {"work": (0, 1, 2, 3, 4, 5, 6, 7), "n": 0}

        def work_bank(shape, dtype, name):
            banks = state["work"]
            b = banks[state["n"] % len(banks)]
            state["n"] = state["n"] + 1
            return psum.tile(shape, dtype, name=name, tag="b%d" % b, bufs=1)

        raw_tiles = {}
        wraw_tiles = {}
        code_tiles = {}
        unit_tiles = {}

        def load_tokens(i):
            t, b = divmod(i, B)
            raw = stream.tile([P, 2, D], BF16, name="raw", tag="raw", bufs=4)
            for s in (0, 1):
                nc.sync.dma_start(out=raw[:, s, :], in_=acts[s][b, t * P : (t + 1) * P, :])
            raw_tiles[i] = raw

        def load_weights(s, piece):
            wr = stream.tile([P, 2, D], BF16, name="wr", tag="wr", bufs=6)
            nc.sync.dma_start(
                out=wr[:],
                in_=weights[s][piece * 256 : (piece + 1) * 256, :].rearrange("(c p) k -> p c k", p=P),
            )
            wraw_tiles[(s, piece)] = wr

        load_tokens(0)
        gpad = const.tile([P, P], BF16, name="gpad", tag="gpad")
        nc.vector.memset(gpad[:], 0.0)
        for s in (0, 1):
            rows = gains[s].rearrange("h o d -> h (o d)")
            for i in (0, 1):
                nc.sync.dma_start(out=gpad[H * s : H * (s + 1), DH * i : DH * (i + 1)], in_=rows)
        load_weights(0, 0)
        load_weights(0, 1)
        load_weights(1, 0)
        load_weights(1, 1)
        load_tokens(1)
        load_weights(0, 2)
        load_weights(0, 3)
        load_weights(1, 2)
        load_weights(1, 3)
        load_tokens(2)
        load_tokens(3)

        ident_f = const.tile([P, P], F32, name="ident_f", tag="ident_f")
        nc.vector.memset(ident_f[:], 0.0)
        make_identity(nc, ident_f[:], nomemset=True)
        ident_b = const.tile([P, P], BF16, name="ident_b", tag="ident_b")
        nc.vector.tensor_copy(out=ident_b[:], in_=ident_f[:])

        one = const.tile([P, 1], F32, name="one", tag="one")
        nc.vector.memset(one[:], 1.0)
        pos_eps2 = const.tile([P, 1], F32, name="pos_eps2", tag="pos_eps2")
        nc.vector.memset(pos_eps2[:], EPS2)
        neg_eps2 = const.tile([P, 1], F32, name="neg_eps2", tag="neg_eps2")
        nc.vector.memset(neg_eps2[:], -EPS2)
        warm = const.tile([P, 1], F32, name="warm", tag="warm")
        nc.scalar.activation(out=warm[:], in_=one[:], func=ACT.Sin)

        wcodes = []
        wscales = []
        for s in (0, 1):
            wc = const.tile([P, 2, H * DH], U32, name="wc%d" % s, tag="wc%d" % s, align_bytes=64)
            ws = const.tile([P, 2, H * DH], U8, name="ws%d" % s, tag="ws%d" % s, align_bytes=64)
            wcodes.append(wc)
            wscales.append(ws)

        frow = const.tile([P, 2, DH], F32, name="frow", tag="frow")
        nc.vector.memset(frow[:, :, 0:1], 1.0)
        for width in (1, 4, 16):
            for m in (width, 2 * width, 3 * width):
                nc.vector.tensor_scalar(
                    out=frow[:, :, m : m + width], in0=frow[:, :, 0:width], scalar1=RATIO**m, scalar2=None, op0=ALU.mult
                )
        fps = work_bank([P, P], F32, "fps")
        nc.tensor.transpose(fps[:], frow[:].rearrange("p a j -> p (a j)"), ident_f[:])

        NB = P + T_TILES - 1
        nb = const.tile([P, NB], F32, name="nb", tag="nb")
        nc.gpsimd.iota(
            nb[:, 0:P], pattern=[[1, P]], base=0, channel_multiplier=0, allow_small_or_imprecise_dtypes=True
        )
        nc.gpsimd.iota(
            nb[:, P:NB],
            pattern=[[P, T_TILES - 1]],
            base=P,
            channel_multiplier=0,
            allow_small_or_imprecise_dtypes=True,
        )
        nbt = const.tile([P, NB], F32, name="nbt", tag="nbt")
        nc.gpsimd.tensor_scalar(
            out=nbt[:], in0=nb[:], scalar1=1.0 / (2.0 * PI), scalar2=0.0, op0=ALU.mult, op1=ALU.add
        )
        y = stream.tile([P, 2, NB], F32, name="y", tag="xp", bufs=5)
        nc.vector.tensor_scalar(out=y[:, 0, :], in0=nbt[:], scalar1=fps[:, 0:1], scalar2=None, op0=ALU.mult)
        nc.vector.tensor_scalar(
            out=y[:, 1, :], in0=nbt[:], scalar1=fps[:, 0:1], scalar2=0.75, op0=ALU.mult, op1=ALU.add
        )
        ki = stream.tile([P, 2, NB], I32, name="ki", tag="xp", bufs=5)
        nc.vector.tensor_copy(out=ki[:], in_=y[:])
        frac = stream.tile([P, 2, NB], F32, name="frac", tag="xp", bufs=5)
        nc.vector.tensor_tensor(out=frac[:], in0=y[:], in1=ki[:], op=ALU.subtract)
        half_sin = stream.tile([P, 2, NB], F32, name="half_sin", tag="yp", bufs=3)
        nc.scalar.activation(out=half_sin[:], in_=frac[:], func=ACT.Sin, scale=PI)
        sq = stream.tile([P, 2, NB], F32, name="sq", tag="yp", bufs=3)
        nc.scalar.activation(out=sq[:], in_=half_sin[:], func=ACT.Square)
        nc.scalar.activation(out=warm[:], in_=sq[:, 0, 0:1], func=ACT.Abs_reciprocal_sqrt, bias=one[:, 0:1])

        trig = const.tile([P, 2, N], F32, name="trig", tag="trig")
        nc.vector.tensor_scalar(
            out=trig[:, :, 0:P], in0=sq[:, :, 0:P], scalar1=-2.0, scalar2=1.0, op0=ALU.mult, op1=ALU.add
        )
        step = const.tile([P, 2, T_TILES - 1], F32, name="step", tag="step")
        nc.vector.tensor_scalar(
            out=step[:], in0=sq[:, :, P:NB], scalar1=-2.0, scalar2=1.0, op0=ALU.mult, op1=ALU.add
        )
        split = const.tile([P, 2, N], BF16, name="split", tag="split")

        def split_columns(lo, hi):
            nc.vector.tensor_copy(out=split[:, :, lo:hi], in_=trig[:, :, lo:hi])
            nc.vector.tensor_tensor(
                out=split[DH:P, :, lo:hi], in0=trig[DH:P, :, lo:hi], in1=split[DH:P, :, lo:hi], op=ALU.subtract
            )

        split_columns(0, P)

        gps = work_bank([P, P], BF16, "gps")
        nc.tensor.transpose(gps[:], gpad[:], ident_b[:])
        gcol = const.tile([P, 2 * H], BF16, name="gcol", tag="gcol")
        nc.vector.tensor_copy(out=gcol[:], in_=gps[:, 0 : 2 * H])
        eye2 = const.tile([P, DH], BF16, name="eye2", tag="eye2")
        nc.gpsimd.tensor_tensor(out=eye2[:], in0=ident_b[:, 0:DH], in1=ident_b[:, DH:P], op=ALU.add)
        diag = []
        for s in (0, 1):
            dm = const.tile([P, H, DH], BF16, name="dm%d" % s, tag="dm%d" % s)
            nc.vector.tensor_tensor(
                out=dm[:],
                in0=eye2[:].unsqueeze(1).to_broadcast([P, H, DH]),
                in1=gcol[:, H * s : H * (s + 1)].unsqueeze(2).to_broadcast([P, H, DH]),
                op=ALU.mult,
            )
            diag.append(dm)

        tables = []
        for t in range(T_TILES):
            tx = const.tile([P, H, 2, DH], F32, name="tx%d" % t, tag="tx%d" % t)
            ty = const.tile([P, H, 2, DH], F32, name="ty%d" % t, tag="ty%d" % t)
            tables.append((tx, ty))

        parts = ((0, 0, 0, 1.0), (1, 0, 1, 1.0), (1, 1, 0, -1.0), (0, 1, 1, 1.0))

        table_banks = {}

        def table_matmul(t, e):
            kind, s, q, sign = parts[e // 2]
            h0 = HEADS * (e % 2)
            ps = work_bank([P, HALF], F32, "tps")
            table_banks[(t, e)] = ps
            nc.tensor.matmul(
                out=ps[:],
                lhsT=split[:, kind, t * P : (t + 1) * P],
                rhs=diag[s][:, h0 : h0 + HEADS, :].rearrange("p h j -> p (h j)"),
                start=True,
                stop=True,
            )

        def table_copy(t, e, on_vector):
            kind, s, q, sign = parts[e // 2]
            h0 = HEADS * (e % 2)
            ps = table_banks[(t, e)]
            if on_vector:
                nc.vector.tensor_scalar(
                    out=tables[t][s][:, h0 : h0 + HEADS, q, :],
                    in0=ps[:].rearrange("p (h j) -> p h j", j=DH),
                    scalar1=sign,
                    scalar2=None,
                    op0=ALU.mult,
                )
            elif sign == 1.0:
                nc.scalar.copy(out=tables[t][s][:, h0 : h0 + HEADS, q, :], in_=ps[:].rearrange("p (h j) -> p h j", j=DH))
            else:
                nc.scalar.activation(
                    out=tables[t][s][:, h0 : h0 + HEADS, q, :],
                    in_=ps[:].rearrange("p (h j) -> p h j", j=DH),
                    func=ACT.Copy,
                    scale=sign,
                )

        group_tiles = {}

        def turn_tokens(i, streams=(0, 1)):
            raw = raw_tiles[i]
            words = raw[:].rearrange("p s k -> p (s k)").bitcast(F32)
            if 0 in streams:
                grouped = stream.tile([P, 2 * D], BF16, name="grouped", tag="grouped", bufs=3, align_bytes=64)
                group_tiles[i] = grouped
            grouped = group_tiles[i]
            gwords = grouped[:].bitcast(F32).rearrange("p (s g r u) -> p s g r u", s=2, g=2, u=2)
            for s in streams:
                bank = work_bank([P, 2, 2, P], F32, "bank")
                for g in (0, 1):
                    for u in (0, 1):
                        lo = 512 * s + 256 * g
                        nc.tensor.transpose(bank[:, g, u, :], words[:, lo + u : lo + 256 : 2], ident_f[:])
                nc.scalar.copy(out=gwords[:, s], in_=bank[:].rearrange("p g u r -> p g r u"))

        bank_tiles = {}

        def turn_start(i, s):
            words = raw_tiles[i][:].rearrange("p s k -> p (s k)").bitcast(F32)
            bank = work_bank([P, 2, 2, P], F32, "bank")
            bank_tiles[(i, s)] = bank
            for g in (0, 1):
                for u in (0, 1):
                    lo = 512 * s + 256 * g
                    nc.tensor.transpose(bank[:, g, u, :], words[:, lo + u : lo + 256 : 2], ident_f[:])

        def turn_finish(i, s, lo_token, hi_token):
            if i not in group_tiles:
                grouped = stream.tile([P, 2 * D], BF16, name="grouped", tag="grouped", bufs=3, align_bytes=64)
                group_tiles[i] = grouped
            gwords = group_tiles[i][:].bitcast(F32).rearrange("p (s g r u) -> p s g r u", s=2, g=2, u=2)
            nc.scalar.copy(
                out=gwords[:, s, :, lo_token:hi_token, :],
                in_=bank_tiles[(i, s)][:, :, :, lo_token:hi_token].rearrange("p g u r -> p g r u"),
            )

        def quantise_tokens(i, streams=(0, 1)):
            grouped = group_tiles[i]
            if i not in code_tiles:
                codes = stream.tile([P, 4 * P], U32, name="codes", tag="codes", bufs=4, align_bytes=64)
                scales = stream.tile([P, 4 * P], U8, name="scales", tag="scales", bufs=4, align_bytes=64)
                code_tiles[i] = (codes, scales)
            codes, scales = code_tiles[i]
            lo = 2 * P * streams[0]
            hi = 2 * P * (streams[-1] + 1)
            nc.vector.quantize_mx(
                out=codes[:, lo:hi].bitcast(E5X4), scales=scales[:, lo:hi], in_=grouped[:, 4 * lo : 4 * hi]
            )

        def prep_weights(s, c, on_vector):
            wgs = []
            for g in (0, 1):
                wg = stream.tile([P, 2, D], BF16, name="wg", tag="wg", bufs=4, align_bytes=64)
                wgs.append(wg)
            for half in (0, 1):
                wr = wraw_tiles[(s, 2 * c + half)]
                words = wr[:].rearrange("p c k -> p (c k)").bitcast(F32)
                for g in (0, 1):
                    wg = wgs[g]
                    bank = work_bank([P, 2, 2, P], F32, "wbank")
                    for r in (0, 1):
                        for u in (0, 1):
                            lo = 512 * r + 256 * g
                            nc.tensor.transpose(bank[:, r, u, :], words[:, lo + u : lo + 256 : 2], ident_f[:])
                    if on_vector and g == 1:
                        nc.vector.tensor_copy(
                            out=wg[:, half, :].bitcast(F32).rearrange("p (c r u) -> p c r u", c=2, u=2),
                            in_=bank[:].rearrange("p c u r -> p c r u"),
                        )
                    else:
                        nc.scalar.copy(
                            out=wg[:, half, :].bitcast(F32).rearrange("p (c r u) -> p c r u", c=2, u=2),
                            in_=bank[:].rearrange("p c u r -> p c r u"),
                        )
            cols = slice(HALF * c, HALF * (c + 1))
            for g in (0, 1):
                nc.vector.quantize_mx(
                    out=wcodes[s][:, g, cols].bitcast(E5X4),
                    scales=wscales[s][:, g, cols],
                    in_=wgs[g][:].rearrange("p h k -> p (h k)"),
                )

        acc_tiles = {}
        norm_tiles = {}

        def matmul_stream(unit, pair, s):
            i, c = unit
            codes, scales = code_tiles[i]
            wcols = slice(HALF * c, HALF * (c + 1))
            bank = psum.tile([P, HALF], F32, name="acc%d" % s, tag="b%d" % (2 * pair + s), bufs=1)
            for g in (0, 1):
                cols = slice((2 * s + g) * P, (2 * s + g + 1) * P)
                nc.tensor.matmul_mx(
                    out=bank[:],
                    lhsT=codes[:, cols].bitcast(E5X4),
                    lhsT_scale=scales[:, cols],
                    rhs=wcodes[s][:, g, wcols].bitcast(E5X4),
                    rhs_scale=wscales[s][:, g, wcols],
                    start=(g == 0),
                    stop=(g == 1),
                )
            acc_tiles.setdefault(unit, {})[s] = bank

        def matmuls(unit, pair):
            for s in (0, 1):
                matmul_stream(unit, pair, s)

        def squares(unit):
            acc = acc_tiles[unit]
            ss = stream.tile([P, 2 * HEADS], F32, name="ss", tag="ss", bufs=4)
            norm_tiles[unit] = ss
            junk = stream.tile([P, 2 * HEADS, DH], BF16, name="junk", tag="junk", bufs=2)
            for s in (0, 1):
                for hh in range(HEADS):
                    nc.scalar.activation(
                        out=junk[:, HEADS * s + hh, :],
                        in_=acc[s][:, DH * hh : DH * (hh + 1)],
                        func=ACT.Square,
                        accum_out=ss[:, HEADS * s + hh : HEADS * s + hh + 1],
                    )

        def clamp(unit):
            floor = stream.tile([P, 2 * HEADS], F32, name="floor", tag="floor", bufs=4)
            nc.scalar.activation(out=floor[:], in_=norm_tiles[unit][:], func=ACT.Relu, bias=neg_eps2[:, 0:1])
            norm_tiles[unit] = floor

        def invert(unit):
            inv = stream.tile([P, 2 * HEADS], F32, name="inv", tag="inv", bufs=4)
            nc.scalar.activation(
                out=inv[:], in_=norm_tiles[unit][:], func=ACT.Abs_reciprocal_sqrt, bias=pos_eps2[:, 0:1]
            )
            unit_tiles[unit] = (acc_tiles[unit], inv)

        def project(unit, pair):
            matmuls(unit, pair)
            squares(unit)
            clamp(unit)
            invert(unit)

        def rotate(unit, next_tile, last, between=None, split_add=False):
            i, c = unit
            t, b = divmod(i, B)
            acc, inv = unit_tiles[unit]
            xp = stream.tile([P, HEADS, 2 * DH], F32, name="xp", tag="xp", bufs=5)
            yp = stream.tile([P, HEADS, 2 * DH], F32, name="yp", tag="yp", bufs=3)
            prod = (xp, yp)
            dest = out[b, HEADS * c : HEADS * (c + 1), t * P : (t + 1) * P, :].rearrange("h n d -> n h d")
            by_head = last or split_add
            order = [(hh, s) for hh in range(HEADS) for s in (0, 1)] if by_head else [(hh, s) for s in (0, 1) for hh in range(HEADS)]
            for n_done, (hh, s) in enumerate(order):
                if n_done == HEADS and between is not None:
                    between()
                if n_done == HEADS and by_head and not last:
                    nc.gpsimd.tensor_tensor(out=xp[:, 0:4, :], in0=xp[:, 0:4, :], in1=yp[:, 0:4, :], op=ALU.add)
                    nc.sync.dma_start(out=dest[:, 0:4, :], in_=xp[:, 0:4, :])
                nc.vector.scalar_tensor_tensor(
                    out=prod[s][:, hh, :].rearrange("p (q j) -> p q j", q=2),
                    in0=acc[s][:, DH * hh : DH * (hh + 1)].unsqueeze(1).to_broadcast([P, 2, DH]),
                    scalar=inv[:, HEADS * s + hh : HEADS * s + hh + 1],
                    in1=tables[t][s][:, HEADS * c + hh, :, :],
                    op0=ALU.mult,
                    op1=ALU.mult,
                )
            if next_tile is not None:
                quantise_tokens(next_tile[0], (next_tile[1],))
            if by_head and not last:
                nc.gpsimd.tensor_tensor(out=xp[:, 4:8, :], in0=xp[:, 4:8, :], in1=yp[:, 4:8, :], op=ALU.add)
                nc.sync.dma_start(out=dest[:, 4:8, :], in_=xp[:, 4:8, :])
            elif not last:
                nc.gpsimd.tensor_tensor(out=xp[:], in0=xp[:], in1=yp[:], op=ALU.add)
                nc.sync.dma_start(out=dest, in_=xp[:])
            if last:
                for hs in (slice(0, 6), slice(6, 8)):
                    nc.vector.tensor_tensor(out=xp[:, hs, :], in0=xp[:, hs, :], in1=yp[:, hs, :], op=ALU.add)
                    nc.sync.dma_start(out=dest[:, hs, :], in_=xp[:, hs, :])

        turn_tokens(0)
        quantise_tokens(0)
        for s in (0, 1):
            prep_weights(s, 0, True)
        turn_tokens(1)
        quantise_tokens(1)
        for e in range(8):
            table_matmul(0, e)
            table_copy(0, e, e % 4 == 0)

        angle_tiles = {}

        def later_angles(t, step_no):
            cols = slice(t * P, (t + 1) * P)
            if step_no == 0:
                by_cos = stream.tile([P, 2, P], F32, name="by_cos", tag="by_cos", bufs=2)
                by_sin = stream.tile([P, 2, P], F32, name="by_sin", tag="by_sin", bufs=2)
                angle_tiles[t] = (by_cos, by_sin)
            by_cos, by_sin = angle_tiles[t]
            if step_no == 0:
                nc.gpsimd.tensor_scalar(
                    out=by_cos[:], in0=trig[:, :, 0:P], scalar1=step[:, 0, t - 1 : t], scalar2=0.0,
                    op0=ALU.mult, op1=ALU.add,
                )
            if step_no == 1:
                nc.gpsimd.tensor_scalar(
                    out=by_sin[:], in0=trig[:, :, 0:P], scalar1=step[:, 1, t - 1 : t], scalar2=0.0,
                    op0=ALU.mult, op1=ALU.add,
                )
            if step_no == 2:
                nc.gpsimd.tensor_tensor(
                    out=trig[:, 0, cols], in0=by_cos[:, 0, :], in1=by_sin[:, 1, :], op=ALU.subtract
                )
            if step_no == 3:
                nc.gpsimd.tensor_tensor(out=trig[:, 1, cols], in0=by_cos[:, 1, :], in1=by_sin[:, 0, :], op=ALU.add)
            if step_no == 4:
                nc.gpsimd.tensor_scalar(
                    out=split[:, :, cols], in0=trig[:, :, cols], scalar1=1.0, scalar2=0.0, op0=ALU.mult, op1=ALU.add
                )
            if step_no == 5:
                nc.gpsimd.tensor_tensor(
                    out=split[DH:P, :, cols], in0=trig[DH:P, :, cols], in1=split[DH:P, :, cols], op=ALU.subtract
                )

        FIRST = 1
        REST = 3
        rest = slice(FIRST * P, (FIRST + REST) * P)
        all_cos = stream.tile([P, REST, 2, P], F32, name="all_cos", tag="xp", bufs=5)
        all_sin = stream.tile([P, REST, 2, P], F32, name="all_sin", tag="xp", bufs=5)
        for t in range(FIRST, FIRST + REST):
            nc.gpsimd.tensor_scalar(
                out=all_cos[:, t - FIRST], in0=trig[:, :, 0:P], scalar1=step[:, 0, t - 1 : t], scalar2=0.0,
                op0=ALU.mult, op1=ALU.add,
            )
            nc.gpsimd.tensor_scalar(
                out=all_sin[:, t - FIRST], in0=trig[:, :, 0:P], scalar1=step[:, 1, t - 1 : t], scalar2=0.0,
                op0=ALU.mult, op1=ALU.add,
            )
        nc.gpsimd.tensor_tensor(
            out=trig[:, 0, rest].rearrange("p (t r) -> p t r", r=P), in0=all_cos[:, :, 0, :], in1=all_sin[:, :, 1, :],
            op=ALU.subtract,
        )
        nc.gpsimd.tensor_tensor(
            out=trig[:, 1, rest].rearrange("p (t r) -> p t r", r=P), in0=all_cos[:, :, 1, :], in1=all_sin[:, :, 0, :],
            op=ALU.add,
        )
        nc.gpsimd.tensor_scalar(
            out=split[:, :, rest], in0=trig[:, :, rest], scalar1=1.0, scalar2=0.0, op0=ALU.mult, op1=ALU.add
        )
        nc.gpsimd.tensor_tensor(
            out=split[DH:P, :, rest], in0=trig[DH:P, :, rest], in1=split[DH:P, :, rest], op=ALU.subtract
        )

        units = [(0, 0), (1, 0), (0, 1), (1, 1)] + [(i, c) for i in range(2, TILES) for c in (0, 1)]
        EARLY = 0

        def pair_of(u):
            return u % 2 if u < EARLY else u % 3

        state["work"] = (6, 7)
        state["n"] = 0
        project(units[0], pair_of(0))
        matmuls(units[1], pair_of(1))
        state["work"] = (4, 5, 6, 7)
        for s in (0, 1):
            prep_weights(s, 1, s == 1)
        state["work"] = (6, 7)
        state["n"] = 0

        def tokens_behind(j):
            return ((j + 6) // 2, 0) if j % 2 == 0 else ((j + 5) // 2, 1)

        def side_start(j):
            i, s = tokens_behind(j)
            if i < TILES:
                turn_start(i, s)
            if j >= 0 and j // 8 + 1 < T_TILES:
                table_matmul(j // 8 + 1, j % 8)

        def step_of(k):
            if k + 2 < len(units):
                matmul_stream(units[k + 2], pair_of(k + 2), 1)
            j = k - 1
            i, s = tokens_behind(j)
            has_tokens = i < TILES
            has_table = j >= 0 and j // 8 + 1 < T_TILES
            scalar_table = has_table and (j % 2 == 0 or j % 4 == 3)
            has_next = k + 1 < len(units)
            if has_next:
                squares(units[k + 1])
            if has_tokens:
                turn_finish(i, s, 0, P if scalar_table else P // 2)
            if has_next:
                clamp(units[k + 1])
            if scalar_table:
                table_copy(j // 8 + 1, j % 8, False)
            elif has_tokens:
                turn_finish(i, s, P // 2, P)
            if has_next:
                invert(units[k + 1])
            due = ((k + 4) // 2, 0) if k % 2 == 0 else ((k + 3) // 2, 1)
            if due[0] >= TILES:
                due = None
            early = (lambda: matmul_stream(units[k + 3], pair_of(k + 3), 0)) if k + 3 < len(units) else None
            rotate(units[k], due, k == len(units) - 1, early, k == len(units) - 2)
            if has_table and not scalar_table:
                table_copy(j // 8 + 1, j % 8, True)
                if k // 4 < 6:
                    later_angles(T_TILES - 1, k // 4)
            if k % 2 == 0 and k // 2 + 4 < TILES:
                load_tokens(k // 2 + 4)
            side_start(k)

        matmul_stream(units[2], pair_of(2), 0)
        turn_tokens(2, (0,))
        side_start(-1)
        pinned = {mybir.EngineType.PE, mybir.EngineType.Activation, mybir.EngineType.DVE, mybir.EngineType.Pool}
        with tc.manual_schedule(engines=pinned):
            for k in range(len(units)):
                step_of(k)
